import numpy as np
import ml_dtypes


def mxq(x, axis, fmt="e4m3"):
    dtype, down = {"e4m3": (ml_dtypes.float8_e4m3fn, 7), "e5m2": (ml_dtypes.float8_e5m2, 14)}[fmt]
    v = np.moveaxis(np.asarray(x, np.float32).astype(ml_dtypes.bfloat16).astype(np.float64), axis, -1)
    blocks = v.reshape(v.shape[:-1] + (-1, 32))
    amax = np.abs(blocks).max(-1, keepdims=True)
    byte = np.maximum(np.where(amax > 0, np.frexp(amax)[1] - 1 + 127, 0) - down, 1)
    scale = np.exp2(byte - 127.0)
    codes = (blocks / scale).astype(np.float32).astype(dtype).astype(np.float64)
    return np.moveaxis((codes * scale).reshape(v.shape), -1, axis)


WIDE = False


def mx_kscale(k):
    if not WIDE:
        return np.ones(k)
    levels = np.array([10, -10, 5, -5, 0])
    a = np.random.permutation(np.resize(levels, k // 512 * 4)).reshape(k // 512, 4)
    idx = np.arange(k)
    return np.exp2(a[idx // 512, idx % 128 // 32])


BF16 = ml_dtypes.bfloat16


def bf(x):
    return np.asarray(x, np.float32).astype(BF16)


def f64(x):
    return np.asarray(x).astype(np.float64)


B, S, D, H, DK, DV, C = 4, 1024, 1024, 4, 128, 128, 512
EPS = 1e-5


def silu(a):
    return a / (1.0 + np.exp(-a))


def setup_inputs():
    s = mx_kscale(D)
    ret = np.random.standard_normal((B, H, S, DV)) + 0.3 * np.random.standard_normal((B, H, S, 1))
    return {"x": bf(np.random.standard_normal((B, S, D)) * s),
            "ret": bf(ret * 0.018 * np.sqrt(DK * S)),
            "Wg": bf(np.random.standard_normal((D, H * DV)) / np.sqrt(D) / s[:, None]),
            "bg": bf(np.random.standard_normal(H * DV) * 0.2),
            "Wo": bf(np.random.standard_normal((H * DV, D)) / np.sqrt(H * DV)),
            "bo": bf(np.random.standard_normal(D) * 0.1)}


def reference(x, ret, Wg, bg, Wo, bo):
    concat = f64(ret).transpose(0, 2, 1, 3).reshape(B * S, H, DV)
    mu = concat.mean(-1, keepdims=True)
    var = ((concat - mu) ** 2).mean(-1, keepdims=True)
    gn = ((concat - mu) / np.sqrt(var + EPS)).reshape(B, S, H * DV)
    gate = silu((mxq(f64(x), 2, "e4m3") @ mxq(f64(Wg), 0, "e4m3")) + f64(bg))
    h = gate * gn
    return (mxq(h, 2, "e4m3") @ mxq(f64(Wo), 0, "e4m3")) + f64(bo)

@@ -1,0 +1,253 @@
+from contextlib import ExitStack
+
+import concourse.mybir as mybir
+from concourse.masks import make_identity
+
+F32 = mybir.dt.float32
+BF16 = mybir.dt.bfloat16
+U32 = mybir.dt.uint32
+U8 = mybir.dt.uint8
+FP8X4 = mybir.dt.float8_e4m3fn_x4
+ALU = mybir.AluOpType
+ACT = mybir.ActivationFunctionType
+
+P = 128
+PACK = 4
+K_PASS = P * PACK
+BANK = 512
+
+BATCH, SEQ, D_MODEL, HEADS, D_HEAD = 4, 1024, 1024, 4, 128
+D_INNER = HEADS * D_HEAD
+EPS = 1e-5
+
+GROUP = 512
+TILES = GROUP // P
+N_GROUPS = BATCH * SEQ // GROUP
+GROUPS_PER_BATCH = SEQ // GROUP
+X_PASSES = D_MODEL // K_PASS
+OUT_HALVES = D_MODEL // BANK
+NORMS = HEADS * TILES
+STATS = 6
+QUARTER = D_HEAD // PACK
+
+FLOPS = 2 * BATCH * SEQ * (D_MODEL * D_INNER + D_INNER * D_MODEL)
+
+
+def tile_gatedmultiscaleretentionlayer_pc_t_kernel(tc, x, ret, Wg, bg, Wo, bo, out):
+    nc = tc.nc
+    x_rows = x.flatten_outer_dims()
+    out_rows = out.flatten_outer_dims()
+
+    with ExitStack() as pools:
+        const = pools.enter_context(tc.tile_pool(name="const", bufs=1))
+        x_pool = pools.enter_context(tc.tile_pool(name="x", bufs=3))
+        ret_pool = pools.enter_context(tc.tile_pool(name="ret", bufs=3))
+        norm_pool = pools.enter_context(tc.tile_pool(name="norm", bufs=3))
+        xq_pool = pools.enter_context(tc.tile_pool(name="xq", bufs=2))
+        gate_pool = pools.enter_context(tc.tile_pool(name="gate", bufs=3))
+        gn_pool = pools.enter_context(tc.tile_pool(name="gn", bufs=4))
+        hq_pool = pools.enter_context(tc.tile_pool(name="hq", bufs=2))
+        o_pool = pools.enter_context(tc.tile_pool(name="o", bufs=8))
+        tp_psum = pools.enter_context(tc.psum_pool(name="tp", bufs=4))
+        mm_psum = pools.enter_context(tc.psum_pool(name="mm", bufs=4))
+
+        x_tiles, ret_tiles, gate_tiles, norm_tiles = {}, {}, {}, {}
+
+        def load_group(j):
+            rows = slice(j * GROUP, (j + 1) * GROUP)
+            x_sb = x_pool.tile([P, TILES, D_MODEL], BF16, name="x_sb")
+            nc.sync.dma_start(out=x_sb[:], in_=x_rows[rows, :].rearrange("(p i) k -> p i k", i=TILES))
+            b, part = divmod(j, GROUPS_PER_BATCH)
+            positions = slice(part * GROUP, (part + 1) * GROUP)
+            ret_sb = ret_pool.tile([P, HEADS, TILES, D_HEAD], BF16, name="ret_sb")
+            nc.sync.dma_start(
+                out=ret_sb[:].rearrange("p h i d -> p h (i d)"),
+                in_=ret[b, :, positions, :].rearrange("h (p i) d -> p h (i d)", i=TILES),
+            )
+            x_tiles[j], ret_tiles[j] = x_sb, ret_sb
+
+        ident = const.tile([P, P], F32, name="ident")
+        make_identity(nc, ident[:])
+        minus_half = const.tile([P, NORMS], F32, name="minus_half")
+        nc.gpsimd.memset(minus_half[:], -0.5)
+
+        wg_raw = const.tile([P, X_PASSES, PACK, D_INNER], BF16, name="wg_raw")
+        nc.sync.dma_start(
+            out=wg_raw[:].rearrange("p g (u e) c -> p (g u) (e c)", e=2),
+            in_=Wg.rearrange("(g u p e) c -> p (g u) (e c)", g=X_PASSES, u=2, e=2),
+        )
+        load_group(0)
+        bg_bf = const.tile([P, PACK], BF16, name="bg_bf")
+        nc.sync.dma_start(out=bg_bf[:], in_=bg.rearrange("(m f) -> m f", f=PACK))
+        wo_raw = const.tile([P, PACK, D_MODEL], BF16, name="wo_raw")
+        nc.sync.dma_start(out=wo_raw[:], in_=Wo.rearrange("(p k) n -> p k n", k=PACK))
+        load_group(1)
+        bo_bf = const.tile([P, D_MODEL], BF16, name="bo_bf")
+        nc.sync.dma_start(out=bo_bf[:], in_=bo.partition_broadcast(P))
+
+        wg_grouped = const.tile([P, X_PASSES, PACK, P, PACK], BF16, name="wg_grouped", align_bytes=64)
+        wg_codes = const.tile([P, X_PASSES, D_INNER], U32, name="wg_codes", align_bytes=64)
+        wg_scales = const.tile([P, X_PASSES, D_INNER], U8, name="wg_scales", align_bytes=64)
+        for g in range(X_PASSES):
+            nc.vector.tensor_copy(
+                out=wg_grouped[:, g, :, :, :], in_=wg_raw[:, g, :, :].rearrange("p k (m f) -> p f m k", f=PACK)
+            )
+        for g in range(X_PASSES):
+            nc.vector.quantize_mx(
+                out=wg_codes[:, g, :].bitcast(FP8X4),
+                scales=wg_scales[:, g, :],
+                in_=wg_grouped[:, g, :, :, :].rearrange("p f m k -> p (f m k)"),
+            )
+        bg_col = const.tile([P, PACK], F32, name="bg_col")
+        nc.vector.tensor_copy(out=bg_col[:], in_=bg_bf[:])
+
+        wo_grouped = const.tile([P, D_MODEL, PACK], BF16, name="wo_grouped", align_bytes=64)
+        wo_codes = const.tile([P, D_MODEL], U32, name="wo_codes", align_bytes=64)
+        wo_scales = const.tile([P, D_MODEL], U8, name="wo_scales", align_bytes=64)
+        nc.scalar.copy(out=wo_grouped[:], in_=wo_raw[:].rearrange("p k n -> p n k"))
+        nc.vector.quantize_mx(
+            out=wo_codes[:].bitcast(FP8X4),
+            scales=wo_scales[:],
+            in_=wo_grouped[:].rearrange("p n k -> p (n k)"),
+        )
+        bo_f32 = const.tile([P, D_MODEL], F32, name="bo_f32")
+        nc.gpsimd.tensor_copy(out=bo_f32[:], in_=bo_bf[:])
+
+        def norm_stage(j):
+            ret_sb = ret_tiles[j]
+            stats = norm_pool.tile([P, NORMS, STATS], F32, name="stats")
+            for h in range(HEADS):
+                for i in range(TILES):
+                    nc.vector.bn_stats(out=stats[:, h * TILES + i, :], in_=ret_sb[:, h, i, :])
+            mean_e, ssd_e, mean_o, ssd_o = stats[:, :, 1], stats[:, :, 2], stats[:, :, 4], stats[:, :, 5]
+            mean_sum = norm_pool.tile([P, NORMS], F32, name="mean_sum")
+            nc.vector.tensor_tensor(out=mean_sum[:], in0=mean_e, in1=mean_o, op=ALU.add)
+            mean_gap = norm_pool.tile([P, NORMS], F32, name="mean_gap")
+            nc.vector.tensor_tensor(out=mean_gap[:], in0=mean_e, in1=mean_o, op=ALU.subtract)
+            gap_sq = norm_pool.tile([P, NORMS], F32, name="gap_sq")
+            nc.vector.tensor_tensor(out=gap_sq[:], in0=mean_gap[:], in1=mean_gap[:], op=ALU.mult)
+            ssd_halves = norm_pool.tile([P, NORMS], F32, name="ssd_halves")
+            nc.vector.tensor_tensor(out=ssd_halves[:], in0=ssd_e, in1=ssd_o, op=ALU.add)
+            ssd = norm_pool.tile([P, NORMS], F32, name="ssd")
+            nc.vector.scalar_tensor_tensor(
+                out=ssd[:], in0=gap_sq[:], scalar=D_HEAD / 4.0, in1=ssd_halves[:], op0=ALU.mult, op1=ALU.add
+            )
+            var_eps = norm_pool.tile([P, NORMS], F32, name="var_eps")
+            nc.gpsimd.tensor_scalar(
+                out=var_eps[:], in0=ssd[:], scalar1=1.0 / D_HEAD, scalar2=EPS, op0=ALU.mult, op1=ALU.add
+            )
+            minus_mean = norm_pool.tile([P, NORMS], F32, name="minus_mean")
+            nc.gpsimd.tensor_scalar(
+                out=minus_mean[:], in0=mean_sum[:], scalar1=-0.5, scalar2=0.0, op0=ALU.mult, op1=ALU.add
+            )
+            rstd = norm_pool.tile([P, NORMS], F32, name="rstd")
+            nc.gpsimd.tensor_tensor(out=rstd[:], in0=var_eps[:], in1=minus_half[:], op=ALU.pow)
+            shift = norm_pool.tile([P, NORMS], F32, name="shift")
+            nc.gpsimd.tensor_tensor(out=shift[:], in0=minus_mean[:], in1=rstd[:], op=ALU.mult)
+            norm_tiles[j] = (rstd, shift)
+
+        def gate_stage(j):
+            x_words = x_tiles[j][:].bitcast(F32)
+            x_grouped = xq_pool.tile([P, X_PASSES, GROUP, PACK], BF16, name="x_grouped", align_bytes=64)
+            x_grouped_words = x_grouped[:].bitcast(F32)
+            x_codes = xq_pool.tile([P, X_PASSES, GROUP], U32, name="x_codes", align_bytes=64)
+            x_scales = xq_pool.tile([P, X_PASSES, GROUP], U8, name="x_scales", align_bytes=64)
+            for g in range(X_PASSES):
+                for pair in range(TILES // 2):
+                    xT = tp_psum.tile([P, 2, 2 * P], F32, name="xT", tag="tp")
+                    for r in range(2):
+                        for u in range(2):
+                            first = (2 * g + u) * P
+                            nc.tensor.transpose(
+                                out=xT[:, u, r * P : (r + 1) * P],
+                                in_=x_words[:, 2 * pair + r, first : first + P],
+                                identity=ident[:],
+                            )
+                    nc.scalar.copy(
+                        out=x_grouped_words[:, g, pair * 2 * P : (pair + 1) * 2 * P, :],
+                        in_=xT[:].rearrange("p u s -> p s u"),
+                    )
+                nc.vector.quantize_mx(
+                    out=x_codes[:, g, :].bitcast(FP8X4),
+                    scales=x_scales[:, g, :],
+                    in_=x_grouped[:, g, :, :].rearrange("p s k -> p (s k)"),
+                )
+            gate = gate_pool.tile([P, PACK, GROUP], F32, name="gate")
+            for f in range(PACK):
+                features = slice(f * P, (f + 1) * P)
+                z = mm_psum.tile([P, GROUP], F32, name="z", tag="mm")
+                for g in range(X_PASSES):
+                    nc.tensor.matmul_mx(
+                        out=z[:],
+                        lhsT=wg_codes[:, g, features].bitcast(FP8X4),
+                        lhsT_scale=wg_scales[:, g, features],
+                        rhs=x_codes[:, g, :].bitcast(FP8X4),
+                        rhs_scale=x_scales[:, g, :],
+                        start=(g == 0),
+                        stop=(g == X_PASSES - 1),
+                    )
+                nc.scalar.activation(out=gate[:, f, :], in_=z[:], func=ACT.Silu, bias=bg_col[:, f : f + 1], scale=1.0)
+            gate_tiles[j] = gate
+
+        def out_stage(j):
+            ret_sb, gate = ret_tiles[j], gate_tiles[j]
+            rstd, shift = norm_tiles[j]
+            h_grouped = hq_pool.tile([P, GROUP, PACK], BF16, name="h_grouped", align_bytes=64)
+            h_codes = hq_pool.tile([P, GROUP], U32, name="h_codes", align_bytes=64)
+            h_scales = hq_pool.tile([P, GROUP], U8, name="h_scales", align_bytes=64)
+            for i in range(TILES):
+                columns = slice(i * P, (i + 1) * P)
+                gn = gn_pool.tile([P, PACK, P], F32, name="gn")
+                for h in range(HEADS):
+                    norm = h * TILES + i
+                    nc.scalar.activation(
+                        out=gn[:, :, h * QUARTER : (h + 1) * QUARTER],
+                        in_=ret_sb[:, h, i, :].rearrange("p (m f) -> p f m", f=PACK),
+                        func=ACT.Identity,
+                        scale=rstd[:, norm : norm + 1],
+                        bias=shift[:, norm : norm + 1],
+                    )
+                gnT = tp_psum.tile([P, PACK, P], F32, name="gnT", tag="tp")
+                for f in range(PACK):
+                    nc.tensor.transpose(out=gnT[:, f, :], in_=gn[:, f, :], identity=ident[:])
+                nc.vector.tensor_tensor(
+                    out=h_grouped[:, columns, :],
+                    in0=gnT[:].rearrange("p f s -> p s f"),
+                    in1=gate[:, :, columns].rearrange("p f s -> p s f"),
+                    op=ALU.mult,
+                )
+            nc.vector.quantize_mx(
+                out=h_codes[:].bitcast(FP8X4), scales=h_scales[:], in_=h_grouped[:].rearrange("p s k -> p (s k)")
+            )
+            group_rows = out_rows[j * GROUP : (j + 1) * GROUP, :].rearrange("(p i) n -> p i n", i=TILES)
+            for i in range(TILES):
+                columns = slice(i * P, (i + 1) * P)
+                o_sb = o_pool.tile([P, D_MODEL], F32, name="o_sb")
+                for n in range(OUT_HALVES):
+                    half = slice(n * BANK, (n + 1) * BANK)
+                    o_ps = mm_psum.tile([P, BANK], F32, name="o_ps", tag="mm")
+                    nc.tensor.matmul_mx(
+                        out=o_ps[:],
+                        lhsT=h_codes[:, columns].bitcast(FP8X4),
+                        lhsT_scale=h_scales[:, columns],
+                        rhs=wo_codes[:, half].bitcast(FP8X4),
+                        rhs_scale=wo_scales[:, half],
+                        start=True,
+                        stop=True,
+                    )
+                    if n == 0:
+                        nc.vector.tensor_tensor(out=o_sb[:, half], in0=o_ps[:], in1=bo_f32[:, half], op=ALU.add)
+                    else:
+                        nc.scalar.copy(out=o_sb[:, half], in_=o_ps[:])
+                        nc.gpsimd.tensor_tensor(out=o_sb[:, half], in0=o_sb[:, half], in1=bo_f32[:, half], op=ALU.add)
+                nc.sync.dma_start(out=group_rows[:, i, :], in_=o_sb[:])
+
+        norm_stage(0)
+        gate_stage(0)
+        for j in range(N_GROUPS):
+            if j + 2 < N_GROUPS:
+                load_group(j + 2)
+            if j + 1 < N_GROUPS:
+                norm_stage(j + 1)
+                gate_stage(j + 1)
+            out_stage(j)

@@ -29,6 +29,10 @@ OUT_HALVES = D_MODEL // BANK
 NORMS = HEADS * TILES
 STATS = 6
 QUARTER = D_HEAD // PACK
+PAIR = 2
+N_PAIRS = BATCH * SEQ // (PAIR * P)
+PAIRS_PER_GROUP = TILES // PAIR
+WO_SLICE = D_MODEL // N_GROUPS
 
 FLOPS = 2 * BATCH * SEQ * (D_MODEL * D_INNER + D_INNER * D_MODEL)
 
@@ -38,216 +42,285 @@ def tile_gatedmultiscaleretentionlayer_pc_t_kernel(tc, x, ret, Wg, bg, Wo, bo, o
     x_rows = x.flatten_outer_dims()
     out_rows = out.flatten_outer_dims()
 
-    with ExitStack() as pools:
-        const = pools.enter_context(tc.tile_pool(name="const", bufs=1))
-        x_pool = pools.enter_context(tc.tile_pool(name="x", bufs=3))
-        ret_pool = pools.enter_context(tc.tile_pool(name="ret", bufs=3))
-        norm_pool = pools.enter_context(tc.tile_pool(name="norm", bufs=3))
-        xq_pool = pools.enter_context(tc.tile_pool(name="xq", bufs=2))
-        gate_pool = pools.enter_context(tc.tile_pool(name="gate", bufs=3))
-        gn_pool = pools.enter_context(tc.tile_pool(name="gn", bufs=4))
-        hq_pool = pools.enter_context(tc.tile_pool(name="hq", bufs=2))
-        o_pool = pools.enter_context(tc.tile_pool(name="o", bufs=8))
-        tp_psum = pools.enter_context(tc.psum_pool(name="tp", bufs=4))
-        mm_psum = pools.enter_context(tc.psum_pool(name="mm", bufs=4))
-
-        x_tiles, ret_tiles, gate_tiles, norm_tiles = {}, {}, {}, {}
-
-        def load_group(j):
-            rows = slice(j * GROUP, (j + 1) * GROUP)
-            x_sb = x_pool.tile([P, TILES, D_MODEL], BF16, name="x_sb")
-            nc.sync.dma_start(out=x_sb[:], in_=x_rows[rows, :].rearrange("(p i) k -> p i k", i=TILES))
-            b, part = divmod(j, GROUPS_PER_BATCH)
-            positions = slice(part * GROUP, (part + 1) * GROUP)
-            ret_sb = ret_pool.tile([P, HEADS, TILES, D_HEAD], BF16, name="ret_sb")
-            nc.sync.dma_start(
-                out=ret_sb[:].rearrange("p h i d -> p h (i d)"),
-                in_=ret[b, :, positions, :].rearrange("h (p i) d -> p h (i d)", i=TILES),
-            )
-            x_tiles[j], ret_tiles[j] = x_sb, ret_sb
+    with ExitStack() as whole:
+        whole.enter_context(tc.manual_schedule())
+        const = whole.enter_context(tc.tile_pool(name="const", bufs=1))
+        ret_pool = whole.enter_context(tc.tile_pool(name="ret", bufs=N_GROUPS))
+        gate_pool = whole.enter_context(tc.tile_pool(name="gate", bufs=N_GROUPS))
+        stat_pool = whole.enter_context(tc.tile_pool(name="stat", bufs=2))
+        tp_psum = whole.enter_context(tc.psum_pool(name="tp", bufs=4))
+        mm_psum = whole.enter_context(tc.psum_pool(name="mm", bufs=4))
 
         ident = const.tile([P, P], F32, name="ident")
         make_identity(nc, ident[:])
         minus_half = const.tile([P, NORMS], F32, name="minus_half")
         nc.gpsimd.memset(minus_half[:], -0.5)
+        table_warmer = const.tile([P, 1], F32, name="table_warmer")
+        nc.scalar.activation(out=table_warmer[:], in_=minus_half[:, 0:1], func=ACT.Silu)
 
-        wg_raw = const.tile([P, X_PASSES, PACK, D_INNER], BF16, name="wg_raw")
-        nc.sync.dma_start(
-            out=wg_raw[:].rearrange("p g (u e) c -> p (g u) (e c)", e=2),
-            in_=Wg.rearrange("(g u p e) c -> p (g u) (e c)", g=X_PASSES, u=2, e=2),
-        )
-        load_group(0)
-        bg_bf = const.tile([P, PACK], BF16, name="bg_bf")
-        nc.sync.dma_start(out=bg_bf[:], in_=bg.rearrange("(m f) -> m f", f=PACK))
-        wo_raw = const.tile([P, PACK, D_MODEL], BF16, name="wo_raw")
-        nc.sync.dma_start(out=wo_raw[:], in_=Wo.rearrange("(p k) n -> p k n", k=PACK))
-        load_group(1)
-        bo_bf = const.tile([P, D_MODEL], BF16, name="bo_bf")
-        nc.sync.dma_start(out=bo_bf[:], in_=bo.partition_broadcast(P))
-
-        wg_grouped = const.tile([P, X_PASSES, PACK, P, PACK], BF16, name="wg_grouped", align_bytes=64)
         wg_codes = const.tile([P, X_PASSES, D_INNER], U32, name="wg_codes", align_bytes=64)
         wg_scales = const.tile([P, X_PASSES, D_INNER], U8, name="wg_scales", align_bytes=64)
-        for g in range(X_PASSES):
-            nc.vector.tensor_copy(
-                out=wg_grouped[:, g, :, :, :], in_=wg_raw[:, g, :, :].rearrange("p k (m f) -> p f m k", f=PACK)
-            )
-        for g in range(X_PASSES):
-            nc.vector.quantize_mx(
-                out=wg_codes[:, g, :].bitcast(FP8X4),
-                scales=wg_scales[:, g, :],
-                in_=wg_grouped[:, g, :, :, :].rearrange("p f m k -> p (f m k)"),
-            )
-        bg_col = const.tile([P, PACK], F32, name="bg_col")
-        nc.vector.tensor_copy(out=bg_col[:], in_=bg_bf[:])
-
-        wo_grouped = const.tile([P, D_MODEL, PACK], BF16, name="wo_grouped", align_bytes=64)
         wo_codes = const.tile([P, D_MODEL], U32, name="wo_codes", align_bytes=64)
         wo_scales = const.tile([P, D_MODEL], U8, name="wo_scales", align_bytes=64)
-        nc.scalar.copy(out=wo_grouped[:], in_=wo_raw[:].rearrange("p k n -> p n k"))
-        nc.vector.quantize_mx(
-            out=wo_codes[:].bitcast(FP8X4),
-            scales=wo_scales[:],
-            in_=wo_grouped[:].rearrange("p n k -> p (n k)"),
-        )
-        bo_f32 = const.tile([P, D_MODEL], F32, name="bo_f32")
-        nc.gpsimd.tensor_copy(out=bo_f32[:], in_=bo_bf[:])
+        bg_col = const.tile([P, PACK], F32, name="bg_col")
+        bo_all = const.tile([P, D_MODEL], BF16, name="bo_all")
+        rstd = const.tile([P, N_GROUPS, NORMS], F32, name="rstd")
+        shift = const.tile([P, N_GROUPS, NORMS], F32, name="shift")
 
-        def norm_stage(j):
-            ret_sb = ret_tiles[j]
-            stats = norm_pool.tile([P, NORMS, STATS], F32, name="stats")
-            for h in range(HEADS):
-                for i in range(TILES):
-                    nc.vector.bn_stats(out=stats[:, h * TILES + i, :], in_=ret_sb[:, h, i, :])
-            mean_e, ssd_e, mean_o, ssd_o = stats[:, :, 1], stats[:, :, 2], stats[:, :, 4], stats[:, :, 5]
-            mean_sum = norm_pool.tile([P, NORMS], F32, name="mean_sum")
-            nc.vector.tensor_tensor(out=mean_sum[:], in0=mean_e, in1=mean_o, op=ALU.add)
-            mean_gap = norm_pool.tile([P, NORMS], F32, name="mean_gap")
-            nc.vector.tensor_tensor(out=mean_gap[:], in0=mean_e, in1=mean_o, op=ALU.subtract)
-            gap_sq = norm_pool.tile([P, NORMS], F32, name="gap_sq")
-            nc.vector.tensor_tensor(out=gap_sq[:], in0=mean_gap[:], in1=mean_gap[:], op=ALU.mult)
-            ssd_halves = norm_pool.tile([P, NORMS], F32, name="ssd_halves")
-            nc.vector.tensor_tensor(out=ssd_halves[:], in0=ssd_e, in1=ssd_o, op=ALU.add)
-            ssd = norm_pool.tile([P, NORMS], F32, name="ssd")
-            nc.vector.scalar_tensor_tensor(
-                out=ssd[:], in0=gap_sq[:], scalar=D_HEAD / 4.0, in1=ssd_halves[:], op0=ALU.mult, op1=ALU.add
-            )
-            var_eps = norm_pool.tile([P, NORMS], F32, name="var_eps")
-            nc.gpsimd.tensor_scalar(
-                out=var_eps[:], in0=ssd[:], scalar1=1.0 / D_HEAD, scalar2=EPS, op0=ALU.mult, op1=ALU.add
-            )
-            minus_mean = norm_pool.tile([P, NORMS], F32, name="minus_mean")
-            nc.gpsimd.tensor_scalar(
-                out=minus_mean[:], in0=mean_sum[:], scalar1=-0.5, scalar2=0.0, op0=ALU.mult, op1=ALU.add
-            )
-            rstd = norm_pool.tile([P, NORMS], F32, name="rstd")
-            nc.gpsimd.tensor_tensor(out=rstd[:], in0=var_eps[:], in1=minus_half[:], op=ALU.pow)
-            shift = norm_pool.tile([P, NORMS], F32, name="shift")
-            nc.gpsimd.tensor_tensor(out=shift[:], in0=minus_mean[:], in1=rstd[:], op=ALU.mult)
-            norm_tiles[j] = (rstd, shift)
+        ret_tiles, gate_tiles = {}, {}
 
-        def gate_stage(j):
-            x_words = x_tiles[j][:].bitcast(F32)
-            x_grouped = xq_pool.tile([P, X_PASSES, GROUP, PACK], BF16, name="x_grouped", align_bytes=64)
-            x_grouped_words = x_grouped[:].bitcast(F32)
-            x_codes = xq_pool.tile([P, X_PASSES, GROUP], U32, name="x_codes", align_bytes=64)
-            x_scales = xq_pool.tile([P, X_PASSES, GROUP], U8, name="x_scales", align_bytes=64)
-            for g in range(X_PASSES):
-                for pair in range(TILES // 2):
-                    xT = tp_psum.tile([P, 2, 2 * P], F32, name="xT", tag="tp")
-                    for r in range(2):
-                        for u in range(2):
-                            first = (2 * g + u) * P
-                            nc.tensor.transpose(
-                                out=xT[:, u, r * P : (r + 1) * P],
-                                in_=x_words[:, 2 * pair + r, first : first + P],
-                                identity=ident[:],
-                            )
-                    nc.scalar.copy(
-                        out=x_grouped_words[:, g, pair * 2 * P : (pair + 1) * 2 * P, :],
-                        in_=xT[:].rearrange("p u s -> p s u"),
-                    )
-                nc.vector.quantize_mx(
-                    out=x_codes[:, g, :].bitcast(FP8X4),
-                    scales=x_scales[:, g, :],
-                    in_=x_grouped[:, g, :, :].rearrange("p s k -> p (s k)"),
+        with ExitStack() as part_one:
+            w_pool = part_one.enter_context(tc.tile_pool(name="w", bufs=1))
+            x_pool = part_one.enter_context(tc.tile_pool(name="x", bufs=3))
+            xq_pool = part_one.enter_context(tc.tile_pool(name="xq", bufs=2))
+
+            x_tiles, x_grouped_tiles, x_code_tiles = {}, {}, {}
+
+            def load_group(j):
+                rows = slice(j * GROUP, (j + 1) * GROUP)
+                x_sb = x_pool.tile([P, TILES, D_MODEL], BF16, name="x_sb")
+                nc.sync.dma_start(out=x_sb[:], in_=x_rows[rows, :].rearrange("(p i) k -> p i k", i=TILES))
+                b, part = divmod(j, GROUPS_PER_BATCH)
+                positions = slice(part * GROUP, (part + 1) * GROUP)
+                ret_sb = ret_pool.tile([P, HEADS, TILES, D_HEAD], BF16, name="ret_sb")
+                nc.sync.dma_start(
+                    out=ret_sb[:].rearrange("p h i d -> p h (i d)"),
+                    in_=ret[b, :, positions, :].rearrange("h (p i) d -> p h (i d)", i=TILES),
                 )
-            gate = gate_pool.tile([P, PACK, GROUP], F32, name="gate")
-            for f in range(PACK):
-                features = slice(f * P, (f + 1) * P)
-                z = mm_psum.tile([P, GROUP], F32, name="z", tag="mm")
+                x_tiles[j], ret_tiles[j] = x_sb, ret_sb
+
+            def transpose_x(j):
+                x_words = x_tiles[j][:].bitcast(F32)
+                x_grouped = xq_pool.tile([P, X_PASSES, GROUP, PACK], BF16, name="x_grouped", align_bytes=64)
+                x_grouped_words = x_grouped[:].bitcast(F32)
                 for g in range(X_PASSES):
-                    nc.tensor.matmul_mx(
-                        out=z[:],
-                        lhsT=wg_codes[:, g, features].bitcast(FP8X4),
-                        lhsT_scale=wg_scales[:, g, features],
-                        rhs=x_codes[:, g, :].bitcast(FP8X4),
-                        rhs_scale=x_scales[:, g, :],
-                        start=(g == 0),
-                        stop=(g == X_PASSES - 1),
-                    )
-                nc.scalar.activation(out=gate[:, f, :], in_=z[:], func=ACT.Silu, bias=bg_col[:, f : f + 1], scale=1.0)
-            gate_tiles[j] = gate
+                    for pair in range(PAIRS_PER_GROUP):
+                        xT = tp_psum.tile([P, 2, PAIR * P], F32, name="xT", tag="tp")
+                        for r in range(PAIR):
+                            for u in range(2):
+                                first = (2 * g + u) * P
+                                nc.tensor.transpose(
+                                    out=xT[:, u, r * P : (r + 1) * P],
+                                    in_=x_words[:, PAIR * pair + r, first : first + P],
+                                    identity=ident[:],
+                                )
+                        nc.scalar.copy(
+                            out=x_grouped_words[:, g, pair * PAIR * P : (pair + 1) * PAIR * P, :],
+                            in_=xT[:].rearrange("p u s -> p s u"),
+                        )
+                x_grouped_tiles[j] = x_grouped
 
-        def out_stage(j):
-            ret_sb, gate = ret_tiles[j], gate_tiles[j]
-            rstd, shift = norm_tiles[j]
-            h_grouped = hq_pool.tile([P, GROUP, PACK], BF16, name="h_grouped", align_bytes=64)
-            h_codes = hq_pool.tile([P, GROUP], U32, name="h_codes", align_bytes=64)
-            h_scales = hq_pool.tile([P, GROUP], U8, name="h_scales", align_bytes=64)
-            for i in range(TILES):
-                columns = slice(i * P, (i + 1) * P)
-                gn = gn_pool.tile([P, PACK, P], F32, name="gn")
+            def quantise_x(j):
+                x_grouped = x_grouped_tiles[j]
+                x_codes = xq_pool.tile([P, X_PASSES, GROUP], U32, name="x_codes", align_bytes=64)
+                x_scales = xq_pool.tile([P, X_PASSES, GROUP], U8, name="x_scales", align_bytes=64)
+                for g in range(X_PASSES):
+                    nc.vector.quantize_mx(
+                        out=x_codes[:, g, :].bitcast(FP8X4),
+                        scales=x_scales[:, g, :],
+                        in_=x_grouped[:, g, :, :].rearrange("p s k -> p (s k)"),
+                    )
+                x_code_tiles[j] = (x_codes, x_scales)
+
+            def norm_stage(j):
+                ret_sb = ret_tiles[j]
+                stats = stat_pool.tile([P, NORMS, STATS], F32, name="stats")
                 for h in range(HEADS):
-                    norm = h * TILES + i
-                    nc.scalar.activation(
-                        out=gn[:, :, h * QUARTER : (h + 1) * QUARTER],
-                        in_=ret_sb[:, h, i, :].rearrange("p (m f) -> p f m", f=PACK),
-                        func=ACT.Identity,
-                        scale=rstd[:, norm : norm + 1],
-                        bias=shift[:, norm : norm + 1],
-                    )
-                gnT = tp_psum.tile([P, PACK, P], F32, name="gnT", tag="tp")
-                for f in range(PACK):
-                    nc.tensor.transpose(out=gnT[:, f, :], in_=gn[:, f, :], identity=ident[:])
-                nc.vector.tensor_tensor(
-                    out=h_grouped[:, columns, :],
-                    in0=gnT[:].rearrange("p f s -> p s f"),
-                    in1=gate[:, :, columns].rearrange("p f s -> p s f"),
-                    op=ALU.mult,
+                    for i in range(TILES):
+                        nc.vector.bn_stats(out=stats[:, h * TILES + i, :], in_=ret_sb[:, h, i, :])
+                mean_e, ssd_e, mean_o, ssd_o = stats[:, :, 1], stats[:, :, 2], stats[:, :, 4], stats[:, :, 5]
+                mean_sum = stat_pool.tile([P, NORMS], F32, name="mean_sum")
+                nc.vector.tensor_tensor(out=mean_sum[:], in0=mean_e, in1=mean_o, op=ALU.add)
+                mean_gap = stat_pool.tile([P, NORMS], F32, name="mean_gap")
+                nc.vector.tensor_tensor(out=mean_gap[:], in0=mean_e, in1=mean_o, op=ALU.subtract)
+                ssd_halves = stat_pool.tile([P, NORMS], F32, name="ssd_halves")
+                nc.vector.tensor_tensor(out=ssd_halves[:], in0=ssd_e, in1=ssd_o, op=ALU.add)
+                gap_sq = stat_pool.tile([P, NORMS], F32, name="gap_sq")
+                nc.vector.tensor_tensor(out=gap_sq[:], in0=mean_gap[:], in1=mean_gap[:], op=ALU.mult)
+                ssd = stat_pool.tile([P, NORMS], F32, name="ssd")
+                nc.vector.scalar_tensor_tensor(
+                    out=ssd[:], in0=gap_sq[:], scalar=D_HEAD / 4.0, in1=ssd_halves[:], op0=ALU.mult, op1=ALU.add
                 )
-            nc.vector.quantize_mx(
-                out=h_codes[:].bitcast(FP8X4), scales=h_scales[:], in_=h_grouped[:].rearrange("p s k -> p (s k)")
-            )
-            group_rows = out_rows[j * GROUP : (j + 1) * GROUP, :].rearrange("(p i) n -> p i n", i=TILES)
-            for i in range(TILES):
-                columns = slice(i * P, (i + 1) * P)
-                o_sb = o_pool.tile([P, D_MODEL], F32, name="o_sb")
-                for n in range(OUT_HALVES):
-                    half = slice(n * BANK, (n + 1) * BANK)
-                    o_ps = mm_psum.tile([P, BANK], F32, name="o_ps", tag="mm")
-                    nc.tensor.matmul_mx(
-                        out=o_ps[:],
-                        lhsT=h_codes[:, columns].bitcast(FP8X4),
-                        lhsT_scale=h_scales[:, columns],
-                        rhs=wo_codes[:, half].bitcast(FP8X4),
-                        rhs_scale=wo_scales[:, half],
-                        start=True,
-                        stop=True,
-                    )
-                    if n == 0:
-                        nc.vector.tensor_tensor(out=o_sb[:, half], in0=o_ps[:], in1=bo_f32[:, half], op=ALU.add)
-                    else:
-                        nc.scalar.copy(out=o_sb[:, half], in_=o_ps[:])
-                        nc.gpsimd.tensor_tensor(out=o_sb[:, half], in0=o_sb[:, half], in1=bo_f32[:, half], op=ALU.add)
-                nc.sync.dma_start(out=group_rows[:, i, :], in_=o_sb[:])
+                var_eps = stat_pool.tile([P, NORMS], F32, name="var_eps")
+                nc.gpsimd.tensor_scalar(
+                    out=var_eps[:], in0=ssd[:], scalar1=1.0 / D_HEAD, scalar2=EPS, op0=ALU.mult, op1=ALU.add
+                )
+                minus_mean = stat_pool.tile([P, NORMS], F32, name="minus_mean")
+                nc.gpsimd.tensor_scalar(
+                    out=minus_mean[:], in0=mean_sum[:], scalar1=-0.5, scalar2=0.0, op0=ALU.mult, op1=ALU.add
+                )
+                nc.gpsimd.tensor_tensor(out=rstd[:, j, :], in0=var_eps[:], in1=minus_half[:], op=ALU.pow)
+                nc.gpsimd.tensor_tensor(out=shift[:, j, :], in0=minus_mean[:], in1=rstd[:, j, :], op=ALU.mult)
 
-        norm_stage(0)
-        gate_stage(0)
-        for j in range(N_GROUPS):
-            if j + 2 < N_GROUPS:
-                load_group(j + 2)
-            if j + 1 < N_GROUPS:
-                norm_stage(j + 1)
-                gate_stage(j + 1)
-            out_stage(j)
+            def regroup_wo_slice(j):
+                columns = slice(j * WO_SLICE, (j + 1) * WO_SLICE)
+                nc.vector.tensor_copy(
+                    out=wo_grouped[:, columns, :], in_=wo_raw[:, :, columns].rearrange("p k n -> p n k")
+                )
+
+            def quantise_wo_slice(j):
+                columns = slice(j * WO_SLICE, (j + 1) * WO_SLICE)
+                nc.vector.quantize_mx(
+                    out=wo_codes[:, columns].bitcast(FP8X4),
+                    scales=wo_scales[:, columns],
+                    in_=wo_grouped[:, columns, :].rearrange("p n k -> p (n k)"),
+                )
+
+            def gate_stage(j):
+                x_codes, x_scales = x_code_tiles[j]
+                gate = gate_pool.tile([P, PACK, GROUP], F32, name="gate")
+                for f in range(PACK):
+                    features = slice(f * P, (f + 1) * P)
+                    z = mm_psum.tile([P, GROUP], F32, name="z", tag="mm")
+                    for g in range(X_PASSES):
+                        nc.tensor.matmul_mx(
+                            out=z[:],
+                            lhsT=wg_codes[:, g, features].bitcast(FP8X4),
+                            lhsT_scale=wg_scales[:, g, features],
+                            rhs=x_codes[:, g, :].bitcast(FP8X4),
+                            rhs_scale=x_scales[:, g, :],
+                            start=(g == 0),
+                            stop=(g == X_PASSES - 1),
+                        )
+                    nc.scalar.activation(
+                        out=gate[:, f, :], in_=z[:], func=ACT.Silu, bias=bg_col[:, f : f + 1], scale=1.0
+                    )
+                gate_tiles[j] = gate
+
+            wg_raw = w_pool.tile([P, X_PASSES, PACK, D_INNER], BF16, name="wg_raw")
+            nc.sync.dma_start(
+                out=wg_raw[:].rearrange("p g (u e) c -> p (g u) (e c)", e=2),
+                in_=Wg.rearrange("(g u p e) c -> p (g u) (e c)", g=X_PASSES, u=2, e=2),
+            )
+            load_group(0)
+            bg_bf = w_pool.tile([P, PACK], BF16, name="bg_bf")
+            nc.sync.dma_start(out=bg_bf[:], in_=bg.rearrange("(m f) -> m f", f=PACK))
+            load_group(1)
+            wo_raw = w_pool.tile([P, PACK, D_MODEL], BF16, name="wo_raw")
+            nc.sync.dma_start(out=wo_raw[:], in_=Wo.rearrange("(p k) n -> p k n", k=PACK))
+            nc.sync.dma_start(out=bo_all[:], in_=bo.partition_broadcast(P))
+
+            wg_grouped = w_pool.tile([P, X_PASSES, PACK, P, PACK], BF16, name="wg_grouped", align_bytes=64)
+            wo_grouped = w_pool.tile([P, D_MODEL, PACK], BF16, name="wo_grouped", align_bytes=64)
+            for g in range(X_PASSES):
+                nc.vector.tensor_copy(
+                    out=wg_grouped[:, g, :, :, :], in_=wg_raw[:, g, :, :].rearrange("p k (m f) -> p f m k", f=PACK)
+                )
+            for g in range(X_PASSES):
+                nc.vector.quantize_mx(
+                    out=wg_codes[:, g, :].bitcast(FP8X4),
+                    scales=wg_scales[:, g, :],
+                    in_=wg_grouped[:, g, :, :, :].rearrange("p f m k -> p (f m k)"),
+                )
+            nc.vector.tensor_copy(out=bg_col[:], in_=bg_bf[:])
+
+            transpose_x(0)
+            quantise_x(0)
+            for j in range(N_GROUPS):
+                if j + 2 < N_GROUPS:
+                    load_group(j + 2)
+                if j + 1 < N_GROUPS:
+                    transpose_x(j + 1)
+                norm_stage(j)
+                regroup_wo_slice(j)
+                if j + 1 < N_GROUPS:
+                    quantise_x(j + 1)
+                quantise_wo_slice(j)
+                gate_stage(j)
+
+        with ExitStack() as part_two:
+            gn_pool = part_two.enter_context(tc.tile_pool(name="gn", bufs=3 * PAIR))
+            hq_pool = part_two.enter_context(tc.tile_pool(name="hq", bufs=3))
+            o_pool = part_two.enter_context(tc.tile_pool(name="o", bufs=4 * PAIR))
+
+            gn_tiles, gnT_tiles, h_grouped_tiles, h_code_tiles = {}, {}, {}, {}
+
+            def tiles_of(r):
+                j, part = divmod(r, PAIRS_PER_GROUP)
+                return j, range(part * PAIR, (part + 1) * PAIR)
+
+            def normalise(r):
+                j, tiles = tiles_of(r)
+                for t, i in enumerate(tiles):
+                    gn = gn_pool.tile([P, PACK, P], F32, name="gn")
+                    for h in range(HEADS):
+                        norm = h * TILES + i
+                        nc.scalar.activation(
+                            out=gn[:, :, h * QUARTER : (h + 1) * QUARTER],
+                            in_=ret_tiles[j][:, h, i, :].rearrange("p (m f) -> p f m", f=PACK),
+                            func=ACT.Identity,
+                            scale=rstd[:, j, norm : norm + 1],
+                            bias=shift[:, j, norm : norm + 1],
+                        )
+                    gn_tiles[r, t] = gn
+
+            def transpose_gn(r):
+                for t in range(PAIR):
+                    gnT = tp_psum.tile([P, PACK, P], F32, name="gnT", tag="tp")
+                    for f in range(PACK):
+                        nc.tensor.transpose(out=gnT[:, f, :], in_=gn_tiles[r, t][:, f, :], identity=ident[:])
+                    gnT_tiles[r, t] = gnT
+
+            def multiply(r):
+                j, tiles = tiles_of(r)
+                h_grouped = hq_pool.tile([P, PAIR * P, PACK], BF16, name="h_grouped", align_bytes=64)
+                for t, i in enumerate(tiles):
+                    nc.vector.tensor_tensor(
+                        out=h_grouped[:, t * P : (t + 1) * P, :],
+                        in0=gnT_tiles[r, t][:].rearrange("p f s -> p s f"),
+                        in1=gate_tiles[j][:, :, i * P : (i + 1) * P].rearrange("p f s -> p s f"),
+                        op=ALU.mult,
+                    )
+                h_grouped_tiles[r] = h_grouped
+
+            def quantise_h(r):
+                h_grouped = h_grouped_tiles[r]
+                h_codes = hq_pool.tile([P, PAIR * P], U32, name="h_codes", align_bytes=64)
+                h_scales = hq_pool.tile([P, PAIR * P], U8, name="h_scales", align_bytes=64)
+                nc.vector.quantize_mx(
+                    out=h_codes[:].bitcast(FP8X4), scales=h_scales[:], in_=h_grouped[:].rearrange("p s k -> p (s k)")
+                )
+                h_code_tiles[r] = (h_codes, h_scales)
+
+            def project(r):
+                j, tiles = tiles_of(r)
+                h_codes, h_scales = h_code_tiles[r]
+                group_rows = out_rows[j * GROUP : (j + 1) * GROUP, :].rearrange("(p i) n -> p i n", i=TILES)
+                for t, i in enumerate(tiles):
+                    columns = slice(t * P, (t + 1) * P)
+                    o_sb = o_pool.tile([P, D_MODEL], F32, name="o_sb")
+                    for n in range(OUT_HALVES):
+                        half = slice(n * BANK, (n + 1) * BANK)
+                        o_ps = mm_psum.tile([P, BANK], F32, name="o_ps", tag="mm")
+                        nc.tensor.matmul_mx(
+                            out=o_ps[:],
+                            lhsT=h_codes[:, columns].bitcast(FP8X4),
+                            lhsT_scale=h_scales[:, columns],
+                            rhs=wo_codes[:, half].bitcast(FP8X4),
+                            rhs_scale=wo_scales[:, half],
+                            start=True,
+                            stop=True,
+                        )
+                        if n == 0:
+                            nc.vector.tensor_tensor(out=o_sb[:, half], in0=o_ps[:], in1=bo_all[:, half], op=ALU.add)
+                        else:
+                            nc.scalar.copy(out=o_sb[:, half], in_=o_ps[:])
+                            nc.gpsimd.tensor_tensor(
+                                out=o_sb[:, half], in0=o_sb[:, half], in1=bo_all[:, half], op=ALU.add
+                            )
+                    nc.sync.dma_start(out=group_rows[:, i, :], in_=o_sb[:])
+
+            normalise(0)
+            normalise(1)
+            transpose_gn(0)
+            multiply(0)
+            quantise_h(0)
+            for r in range(N_PAIRS):
+                if r + 2 < N_PAIRS:
+                    normalise(r + 2)
+                if r + 1 < N_PAIRS:
+                    transpose_gn(r + 1)
+                    multiply(r + 1)
+                project(r)
+                if r + 1 < N_PAIRS:
+                    quantise_h(r + 1)

@@ -32,6 +32,7 @@ QUARTER = D_HEAD // PACK
 PAIR = 2
 N_PAIRS = BATCH * SEQ // (PAIR * P)
 PAIRS_PER_GROUP = TILES // PAIR
+FEATURE_TILES_PER_RUN = PACK // X_PASSES
 WO_SLICE = D_MODEL // N_GROUPS
 
 FLOPS = 2 * BATCH * SEQ * (D_MODEL * D_INNER + D_INNER * D_MODEL)
@@ -45,8 +46,6 @@ def tile_gatedmultiscaleretentionlayer_pc_t_kernel(tc, x, ret, Wg, bg, Wo, bo, o
     with ExitStack() as whole:
         whole.enter_context(tc.manual_schedule())
         const = whole.enter_context(tc.tile_pool(name="const", bufs=1))
-        ret_pool = whole.enter_context(tc.tile_pool(name="ret", bufs=N_GROUPS))
-        gate_pool = whole.enter_context(tc.tile_pool(name="gate", bufs=N_GROUPS))
         stat_pool = whole.enter_context(tc.tile_pool(name="stat", bufs=2))
         tp_psum = whole.enter_context(tc.psum_pool(name="tp", bufs=4))
         mm_psum = whole.enter_context(tc.psum_pool(name="mm", bufs=4))
@@ -64,15 +63,15 @@ def tile_gatedmultiscaleretentionlayer_pc_t_kernel(tc, x, ret, Wg, bg, Wo, bo, o
         wo_scales = const.tile([P, D_MODEL], U8, name="wo_scales", align_bytes=64)
         bg_col = const.tile([P, PACK], F32, name="bg_col")
         bo_all = const.tile([P, D_MODEL], BF16, name="bo_all")
+        ret_all = const.tile([P, N_GROUPS, HEADS, TILES, D_HEAD], BF16, name="ret_all")
+        gate_all = const.tile([P, N_GROUPS, PACK, GROUP], F32, name="gate_all")
         rstd = const.tile([P, N_GROUPS, NORMS], F32, name="rstd")
         shift = const.tile([P, N_GROUPS, NORMS], F32, name="shift")
-
-        ret_tiles, gate_tiles = {}, {}
 
         with ExitStack() as part_one:
             w_pool = part_one.enter_context(tc.tile_pool(name="w", bufs=1))
             x_pool = part_one.enter_context(tc.tile_pool(name="x", bufs=3))
-            xq_pool = part_one.enter_context(tc.tile_pool(name="xq", bufs=2))
+            xq_pool = part_one.enter_context(tc.tile_pool(name="xq", bufs=2 * X_PASSES))
 
             x_tiles, x_grouped_tiles, x_code_tiles = {}, {}, {}
 
@@ -82,52 +81,65 @@ def tile_gatedmultiscaleretentionlayer_pc_t_kernel(tc, x, ret, Wg, bg, Wo, bo, o
                 nc.sync.dma_start(out=x_sb[:], in_=x_rows[rows, :].rearrange("(p i) k -> p i k", i=TILES))
                 b, part = divmod(j, GROUPS_PER_BATCH)
                 positions = slice(part * GROUP, (part + 1) * GROUP)
-                ret_sb = ret_pool.tile([P, HEADS, TILES, D_HEAD], BF16, name="ret_sb")
                 nc.sync.dma_start(
-                    out=ret_sb[:].rearrange("p h i d -> p h (i d)"),
+                    out=ret_all[:, j, :, :, :].rearrange("p h i d -> p h (i d)"),
                     in_=ret[b, :, positions, :].rearrange("h (p i) d -> p h (i d)", i=TILES),
                 )
-                x_tiles[j], ret_tiles[j] = x_sb, ret_sb
+                x_tiles[j] = x_sb
 
-            def transpose_x(j):
+            def transpose_x(j, g):
                 x_words = x_tiles[j][:].bitcast(F32)
-                x_grouped = xq_pool.tile([P, X_PASSES, GROUP, PACK], BF16, name="x_grouped", align_bytes=64)
+                x_grouped = xq_pool.tile([P, GROUP, PACK], BF16, name="x_grouped", align_bytes=64)
                 x_grouped_words = x_grouped[:].bitcast(F32)
-                for g in range(X_PASSES):
-                    for pair in range(PAIRS_PER_GROUP):
-                        xT = tp_psum.tile([P, 2, PAIR * P], F32, name="xT", tag="tp")
-                        for r in range(PAIR):
-                            for u in range(2):
-                                first = (2 * g + u) * P
-                                nc.tensor.transpose(
-                                    out=xT[:, u, r * P : (r + 1) * P],
-                                    in_=x_words[:, PAIR * pair + r, first : first + P],
-                                    identity=ident[:],
-                                )
-                        nc.scalar.copy(
-                            out=x_grouped_words[:, g, pair * PAIR * P : (pair + 1) * PAIR * P, :],
-                            in_=xT[:].rearrange("p u s -> p s u"),
-                        )
-                x_grouped_tiles[j] = x_grouped
-
-            def quantise_x(j):
-                x_grouped = x_grouped_tiles[j]
-                x_codes = xq_pool.tile([P, X_PASSES, GROUP], U32, name="x_codes", align_bytes=64)
-                x_scales = xq_pool.tile([P, X_PASSES, GROUP], U8, name="x_scales", align_bytes=64)
-                for g in range(X_PASSES):
-                    nc.vector.quantize_mx(
-                        out=x_codes[:, g, :].bitcast(FP8X4),
-                        scales=x_scales[:, g, :],
-                        in_=x_grouped[:, g, :, :].rearrange("p s k -> p (s k)"),
+                for pair in range(PAIRS_PER_GROUP):
+                    xT = tp_psum.tile([P, 2, PAIR * P], F32, name="xT", tag="tp")
+                    for r in range(PAIR):
+                        for u in range(2):
+                            first = (2 * g + u) * P
+                            nc.tensor.transpose(
+                                out=xT[:, u, r * P : (r + 1) * P],
+                                in_=x_words[:, PAIR * pair + r, first : first + P],
+                                identity=ident[:],
+                            )
+                    nc.scalar.copy(
+                        out=x_grouped_words[:, pair * PAIR * P : (pair + 1) * PAIR * P, :],
+                        in_=xT[:].rearrange("p u s -> p s u"),
                     )
-                x_code_tiles[j] = (x_codes, x_scales)
+                x_grouped_tiles[j, g] = x_grouped
+
+            def quantise_x(j, g):
+                x_codes = xq_pool.tile([P, GROUP], U32, name="x_codes", align_bytes=64)
+                x_scales = xq_pool.tile([P, GROUP], U8, name="x_scales", align_bytes=64)
+                nc.vector.quantize_mx(
+                    out=x_codes[:].bitcast(FP8X4),
+                    scales=x_scales[:],
+                    in_=x_grouped_tiles[j, g][:].rearrange("p s k -> p (s k)"),
+                )
+                x_code_tiles[j, g] = (x_codes, x_scales)
+
+            def gate_features(j, f):
+                features = slice(f * P, (f + 1) * P)
+                z = mm_psum.tile([P, GROUP], F32, name="z", tag="mm")
+                for g in range(X_PASSES):
+                    x_codes, x_scales = x_code_tiles[j, g]
+                    nc.tensor.matmul_mx(
+                        out=z[:],
+                        lhsT=wg_codes[:, g, features].bitcast(FP8X4),
+                        lhsT_scale=wg_scales[:, g, features],
+                        rhs=x_codes[:].bitcast(FP8X4),
+                        rhs_scale=x_scales[:],
+                        start=(g == 0),
+                        stop=(g == X_PASSES - 1),
+                    )
+                nc.scalar.activation(
+                    out=gate_all[:, j, f, :], in_=z[:], func=ACT.Silu, bias=bg_col[:, f : f + 1], scale=1.0
+                )
 
             def norm_stage(j):
-                ret_sb = ret_tiles[j]
                 stats = stat_pool.tile([P, NORMS, STATS], F32, name="stats")
                 for h in range(HEADS):
                     for i in range(TILES):
-                        nc.vector.bn_stats(out=stats[:, h * TILES + i, :], in_=ret_sb[:, h, i, :])
+                        nc.vector.bn_stats(out=stats[:, h * TILES + i, :], in_=ret_all[:, j, h, i, :])
                 mean_e, ssd_e, mean_o, ssd_o = stats[:, :, 1], stats[:, :, 2], stats[:, :, 4], stats[:, :, 5]
                 mean_sum = stat_pool.tile([P, NORMS], F32, name="mean_sum")
                 nc.vector.tensor_tensor(out=mean_sum[:], in0=mean_e, in1=mean_o, op=ALU.add)
@@ -166,27 +178,6 @@ def tile_gatedmultiscaleretentionlayer_pc_t_kernel(tc, x, ret, Wg, bg, Wo, bo, o
                     in_=wo_grouped[:, columns, :].rearrange("p n k -> p (n k)"),
                 )
 
-            def gate_stage(j):
-                x_codes, x_scales = x_code_tiles[j]
-                gate = gate_pool.tile([P, PACK, GROUP], F32, name="gate")
-                for f in range(PACK):
-                    features = slice(f * P, (f + 1) * P)
-                    z = mm_psum.tile([P, GROUP], F32, name="z", tag="mm")
-                    for g in range(X_PASSES):
-                        nc.tensor.matmul_mx(
-                            out=z[:],
-                            lhsT=wg_codes[:, g, features].bitcast(FP8X4),
-                            lhsT_scale=wg_scales[:, g, features],
-                            rhs=x_codes[:, g, :].bitcast(FP8X4),
-                            rhs_scale=x_scales[:, g, :],
-                            start=(g == 0),
-                            stop=(g == X_PASSES - 1),
-                        )
-                    nc.scalar.activation(
-                        out=gate[:, f, :], in_=z[:], func=ACT.Silu, bias=bg_col[:, f : f + 1], scale=1.0
-                    )
-                gate_tiles[j] = gate
-
             wg_raw = w_pool.tile([P, X_PASSES, PACK, D_INNER], BF16, name="wg_raw")
             nc.sync.dma_start(
                 out=wg_raw[:].rearrange("p g (u e) c -> p (g u) (e c)", e=2),
@@ -214,19 +205,23 @@ def tile_gatedmultiscaleretentionlayer_pc_t_kernel(tc, x, ret, Wg, bg, Wo, bo, o
                 )
             nc.vector.tensor_copy(out=bg_col[:], in_=bg_bf[:])
 
-            transpose_x(0)
-            quantise_x(0)
+            for g in range(X_PASSES):
+                transpose_x(0, g)
+                quantise_x(0, g)
             for j in range(N_GROUPS):
                 if j + 2 < N_GROUPS:
                     load_group(j + 2)
-                if j + 1 < N_GROUPS:
-                    transpose_x(j + 1)
+                for g in range(X_PASSES):
+                    if j + 1 < N_GROUPS:
+                        transpose_x(j + 1, g)
+                    for f in range(g * FEATURE_TILES_PER_RUN, (g + 1) * FEATURE_TILES_PER_RUN):
+                        gate_features(j, f)
                 norm_stage(j)
                 regroup_wo_slice(j)
                 if j + 1 < N_GROUPS:
-                    quantise_x(j + 1)
+                    for g in range(X_PASSES):
+                        quantise_x(j + 1, g)
                 quantise_wo_slice(j)
-                gate_stage(j)
 
         with ExitStack() as part_two:
             gn_pool = part_two.enter_context(tc.tile_pool(name="gn", bufs=3 * PAIR))
@@ -235,92 +230,90 @@ def tile_gatedmultiscaleretentionlayer_pc_t_kernel(tc, x, ret, Wg, bg, Wo, bo, o
 
             gn_tiles, gnT_tiles, h_grouped_tiles, h_code_tiles = {}, {}, {}, {}
 
-            def tiles_of(r):
+            def place_of(r, t):
                 j, part = divmod(r, PAIRS_PER_GROUP)
-                return j, range(part * PAIR, (part + 1) * PAIR)
+                return j, part * PAIR + t
 
-            def normalise(r):
-                j, tiles = tiles_of(r)
-                for t, i in enumerate(tiles):
-                    gn = gn_pool.tile([P, PACK, P], F32, name="gn")
-                    for h in range(HEADS):
-                        norm = h * TILES + i
-                        nc.scalar.activation(
-                            out=gn[:, :, h * QUARTER : (h + 1) * QUARTER],
-                            in_=ret_tiles[j][:, h, i, :].rearrange("p (m f) -> p f m", f=PACK),
-                            func=ACT.Identity,
-                            scale=rstd[:, j, norm : norm + 1],
-                            bias=shift[:, j, norm : norm + 1],
-                        )
-                    gn_tiles[r, t] = gn
-
-            def transpose_gn(r):
-                for t in range(PAIR):
-                    gnT = tp_psum.tile([P, PACK, P], F32, name="gnT", tag="tp")
-                    for f in range(PACK):
-                        nc.tensor.transpose(out=gnT[:, f, :], in_=gn_tiles[r, t][:, f, :], identity=ident[:])
-                    gnT_tiles[r, t] = gnT
-
-            def multiply(r):
-                j, tiles = tiles_of(r)
-                h_grouped = hq_pool.tile([P, PAIR * P, PACK], BF16, name="h_grouped", align_bytes=64)
-                for t, i in enumerate(tiles):
-                    nc.vector.tensor_tensor(
-                        out=h_grouped[:, t * P : (t + 1) * P, :],
-                        in0=gnT_tiles[r, t][:].rearrange("p f s -> p s f"),
-                        in1=gate_tiles[j][:, :, i * P : (i + 1) * P].rearrange("p f s -> p s f"),
-                        op=ALU.mult,
+            def normalise(r, t):
+                j, i = place_of(r, t)
+                gn = gn_pool.tile([P, PACK, P], F32, name="gn")
+                for h in range(HEADS):
+                    norm = h * TILES + i
+                    nc.scalar.activation(
+                        out=gn[:, :, h * QUARTER : (h + 1) * QUARTER],
+                        in_=ret_all[:, j, h, i, :].rearrange("p (m f) -> p f m", f=PACK),
+                        func=ACT.Identity,
+                        scale=rstd[:, j, norm : norm + 1],
+                        bias=shift[:, j, norm : norm + 1],
                     )
-                h_grouped_tiles[r] = h_grouped
+                gn_tiles[r, t] = gn
+
+            def transpose_gn(r, t):
+                gnT = tp_psum.tile([P, PACK, P], F32, name="gnT", tag="tp")
+                for f in range(PACK):
+                    nc.tensor.transpose(out=gnT[:, f, :], in_=gn_tiles[r, t][:, f, :], identity=ident[:])
+                gnT_tiles[r, t] = gnT
+
+            def multiply(r, t):
+                j, i = place_of(r, t)
+                if t == 0:
+                    h_grouped_tiles[r] = hq_pool.tile([P, PAIR * P, PACK], BF16, name="h_grouped", align_bytes=64)
+                nc.vector.tensor_tensor(
+                    out=h_grouped_tiles[r][:, t * P : (t + 1) * P, :],
+                    in0=gnT_tiles[r, t][:].rearrange("p f s -> p s f"),
+                    in1=gate_all[:, j, :, i * P : (i + 1) * P].rearrange("p f s -> p s f"),
+                    op=ALU.mult,
+                )
 
             def quantise_h(r):
-                h_grouped = h_grouped_tiles[r]
                 h_codes = hq_pool.tile([P, PAIR * P], U32, name="h_codes", align_bytes=64)
                 h_scales = hq_pool.tile([P, PAIR * P], U8, name="h_scales", align_bytes=64)
                 nc.vector.quantize_mx(
-                    out=h_codes[:].bitcast(FP8X4), scales=h_scales[:], in_=h_grouped[:].rearrange("p s k -> p (s k)")
+                    out=h_codes[:].bitcast(FP8X4),
+                    scales=h_scales[:],
+                    in_=h_grouped_tiles[r][:].rearrange("p s k -> p (s k)"),
                 )
                 h_code_tiles[r] = (h_codes, h_scales)
 
-            def project(r):
-                j, tiles = tiles_of(r)
+            def project(r, t):
+                j, i = place_of(r, t)
                 h_codes, h_scales = h_code_tiles[r]
+                columns = slice(t * P, (t + 1) * P)
+                o_sb = o_pool.tile([P, D_MODEL], F32, name="o_sb")
+                for n in range(OUT_HALVES):
+                    half = slice(n * BANK, (n + 1) * BANK)
+                    o_ps = mm_psum.tile([P, BANK], F32, name="o_ps", tag="mm")
+                    nc.tensor.matmul_mx(
+                        out=o_ps[:],
+                        lhsT=h_codes[:, columns].bitcast(FP8X4),
+                        lhsT_scale=h_scales[:, columns],
+                        rhs=wo_codes[:, half].bitcast(FP8X4),
+                        rhs_scale=wo_scales[:, half],
+                        start=True,
+                        stop=True,
+                    )
+                    if n == 0:
+                        nc.vector.tensor_tensor(out=o_sb[:, half], in0=o_ps[:], in1=bo_all[:, half], op=ALU.add)
+                    else:
+                        nc.scalar.copy(out=o_sb[:, half], in_=o_ps[:])
+                        nc.gpsimd.tensor_tensor(out=o_sb[:, half], in0=o_sb[:, half], in1=bo_all[:, half], op=ALU.add)
                 group_rows = out_rows[j * GROUP : (j + 1) * GROUP, :].rearrange("(p i) n -> p i n", i=TILES)
-                for t, i in enumerate(tiles):
-                    columns = slice(t * P, (t + 1) * P)
-                    o_sb = o_pool.tile([P, D_MODEL], F32, name="o_sb")
-                    for n in range(OUT_HALVES):
-                        half = slice(n * BANK, (n + 1) * BANK)
-                        o_ps = mm_psum.tile([P, BANK], F32, name="o_ps", tag="mm")
-                        nc.tensor.matmul_mx(
-                            out=o_ps[:],
-                            lhsT=h_codes[:, columns].bitcast(FP8X4),
-                            lhsT_scale=h_scales[:, columns],
-                            rhs=wo_codes[:, half].bitcast(FP8X4),
-                            rhs_scale=wo_scales[:, half],
-                            start=True,
-                            stop=True,
-                        )
-                        if n == 0:
-                            nc.vector.tensor_tensor(out=o_sb[:, half], in0=o_ps[:], in1=bo_all[:, half], op=ALU.add)
-                        else:
-                            nc.scalar.copy(out=o_sb[:, half], in_=o_ps[:])
-                            nc.gpsimd.tensor_tensor(
-                                out=o_sb[:, half], in0=o_sb[:, half], in1=bo_all[:, half], op=ALU.add
-                            )
-                    nc.sync.dma_start(out=group_rows[:, i, :], in_=o_sb[:])
+                nc.sync.dma_start(out=group_rows[:, i, :], in_=o_sb[:])
 
-            normalise(0)
-            normalise(1)
-            transpose_gn(0)
-            multiply(0)
+            for t in range(PAIR):
+                normalise(0, t)
+            for t in range(PAIR):
+                normalise(1, t)
+                transpose_gn(0, t)
+                multiply(0, t)
             quantise_h(0)
             for r in range(N_PAIRS):
-                if r + 2 < N_PAIRS:
-                    normalise(r + 2)
-                if r + 1 < N_PAIRS:
-                    transpose_gn(r + 1)
-                    multiply(r + 1)
-                project(r)
+                for t in range(PAIR):
+                    if r + 2 < N_PAIRS:
+                        normalise(r + 2, t)
+                    if r + 1 < N_PAIRS:
+                        transpose_gn(r + 1, t)
+                        multiply(r + 1, t)
+                    project(r, t)
                 if r + 1 < N_PAIRS:
                     quantise_h(r + 1)

@@ -25,7 +25,6 @@ TILES = GROUP // P
 N_GROUPS = BATCH * SEQ // GROUP
 GROUPS_PER_BATCH = SEQ // GROUP
 X_PASSES = D_MODEL // K_PASS
-OUT_HALVES = D_MODEL // BANK
 NORMS = HEADS * TILES
 STATS = 6
 QUARTER = D_HEAD // PACK
@@ -280,9 +279,10 @@ def tile_gatedmultiscaleretentionlayer_pc_t_kernel(tc, x, ret, Wg, bg, Wo, bo, o
                 h_codes, h_scales = h_code_tiles[r]
                 columns = slice(t * P, (t + 1) * P)
                 o_sb = o_pool.tile([P, D_MODEL], F32, name="o_sb")
-                for n in range(OUT_HALVES):
-                    half = slice(n * BANK, (n + 1) * BANK)
-                    o_ps = mm_psum.tile([P, BANK], F32, name="o_ps", tag="mm")
+                first_ps = mm_psum.tile([P, BANK], F32, name="first_ps", tag="mm")
+                second_ps = mm_psum.tile([P, BANK], F32, name="second_ps", tag="mm")
+                first_half, second_half = slice(0, BANK), slice(BANK, 2 * BANK)
+                for o_ps, half in ((first_ps, first_half), (second_ps, second_half), (first_ps, first_half)):
                     nc.tensor.matmul_mx(
                         out=o_ps[:],
                         lhsT=h_codes[:, columns].bitcast(FP8X4),
@@ -292,11 +292,11 @@ def tile_gatedmultiscaleretentionlayer_pc_t_kernel(tc, x, ret, Wg, bg, Wo, bo, o
                         start=True,
                         stop=True,
                     )
-                    if n == 0:
-                        nc.vector.tensor_tensor(out=o_sb[:, half], in0=o_ps[:], in1=bo_all[:, half], op=ALU.add)
-                    else:
-                        nc.scalar.copy(out=o_sb[:, half], in_=o_ps[:])
-                        nc.gpsimd.tensor_tensor(out=o_sb[:, half], in0=o_sb[:, half], in1=bo_all[:, half], op=ALU.add)
+                nc.scalar.copy(out=o_sb[:, second_half], in_=second_ps[:])
+                nc.gpsimd.tensor_tensor(
+                    out=o_sb[:, second_half], in0=o_sb[:, second_half], in1=bo_all[:, second_half], op=ALU.add
+                )
+                nc.vector.tensor_tensor(out=o_sb[:, first_half], in0=first_ps[:], in1=bo_all[:, first_half], op=ALU.add)
                 group_rows = out_rows[j * GROUP : (j + 1) * GROUP, :].rearrange("(p i) n -> p i n", i=TILES)
                 nc.sync.dma_start(out=group_rows[:, i, :], in_=o_sb[:])
 

@@ -25,11 +25,13 @@ TILES = GROUP // P
 N_GROUPS = BATCH * SEQ // GROUP
 GROUPS_PER_BATCH = SEQ // GROUP
 X_PASSES = D_MODEL // K_PASS
+OUT_HALVES = D_MODEL // BANK
 NORMS = HEADS * TILES
 STATS = 6
 QUARTER = D_HEAD // PACK
 PAIR = 2
-N_PAIRS = BATCH * SEQ // (PAIR * P)
+N_TILES = BATCH * SEQ // P
+NORMALISE_AHEAD, TRANSPOSE_AHEAD, MULTIPLY_AHEAD, PROJECT_AHEAD = 7, 5, 4, 1
 PAIRS_PER_GROUP = TILES // PAIR
 FEATURE_TILES_PER_RUN = PACK // X_PASSES
 WO_SLICE = D_MODEL // N_GROUPS
@@ -223,18 +225,14 @@ def tile_gatedmultiscaleretentionlayer_pc_t_kernel(tc, x, ret, Wg, bg, Wo, bo, o
                 quantise_wo_slice(j)
 
         with ExitStack() as part_two:
-            gn_pool = part_two.enter_context(tc.tile_pool(name="gn", bufs=3 * PAIR))
+            gn_pool = part_two.enter_context(tc.tile_pool(name="gn", bufs=4))
             hq_pool = part_two.enter_context(tc.tile_pool(name="hq", bufs=3))
-            o_pool = part_two.enter_context(tc.tile_pool(name="o", bufs=4 * PAIR))
+            o_pool = part_two.enter_context(tc.tile_pool(name="o", bufs=8))
 
-            gn_tiles, gnT_tiles, h_grouped_tiles, h_code_tiles = {}, {}, {}, {}
+            gn_tiles, gnT_tiles, h_grouped_tiles, h_code_tiles, o_banks = {}, {}, {}, {}, {}
 
-            def place_of(r, t):
-                j, part = divmod(r, PAIRS_PER_GROUP)
-                return j, part * PAIR + t
-
-            def normalise(r, t):
-                j, i = place_of(r, t)
+            def normalise(q):
+                j, i = divmod(q, TILES)
                 gn = gn_pool.tile([P, PACK, P], F32, name="gn")
                 for h in range(HEADS):
                     norm = h * TILES + i
@@ -245,44 +243,43 @@ def tile_gatedmultiscaleretentionlayer_pc_t_kernel(tc, x, ret, Wg, bg, Wo, bo, o
                         scale=rstd[:, j, norm : norm + 1],
                         bias=shift[:, j, norm : norm + 1],
                     )
-                gn_tiles[r, t] = gn
+                gn_tiles[q] = gn
 
-            def transpose_gn(r, t):
+            def transpose_gn(q):
                 gnT = tp_psum.tile([P, PACK, P], F32, name="gnT", tag="tp")
                 for f in range(PACK):
-                    nc.tensor.transpose(out=gnT[:, f, :], in_=gn_tiles[r, t][:, f, :], identity=ident[:])
-                gnT_tiles[r, t] = gnT
+                    nc.tensor.transpose(out=gnT[:, f, :], in_=gn_tiles[q][:, f, :], identity=ident[:])
+                gnT_tiles[q] = gnT
 
-            def multiply(r, t):
-                j, i = place_of(r, t)
+            def multiply(q):
+                j, i = divmod(q, TILES)
+                pair, t = divmod(q, PAIR)
                 if t == 0:
-                    h_grouped_tiles[r] = hq_pool.tile([P, PAIR * P, PACK], BF16, name="h_grouped", align_bytes=64)
+                    h_grouped_tiles[pair] = hq_pool.tile([P, PAIR * P, PACK], BF16, name="h_grouped", align_bytes=64)
                 nc.vector.tensor_tensor(
-                    out=h_grouped_tiles[r][:, t * P : (t + 1) * P, :],
-                    in0=gnT_tiles[r, t][:].rearrange("p f s -> p s f"),
+                    out=h_grouped_tiles[pair][:, t * P : (t + 1) * P, :],
+                    in0=gnT_tiles[q][:].rearrange("p f s -> p s f"),
                     in1=gate_all[:, j, :, i * P : (i + 1) * P].rearrange("p f s -> p s f"),
                     op=ALU.mult,
                 )
 
-            def quantise_h(r):
+            def quantise_h(pair):
                 h_codes = hq_pool.tile([P, PAIR * P], U32, name="h_codes", align_bytes=64)
                 h_scales = hq_pool.tile([P, PAIR * P], U8, name="h_scales", align_bytes=64)
                 nc.vector.quantize_mx(
                     out=h_codes[:].bitcast(FP8X4),
                     scales=h_scales[:],
-                    in_=h_grouped_tiles[r][:].rearrange("p s k -> p (s k)"),
+                    in_=h_grouped_tiles[pair][:].rearrange("p s k -> p (s k)"),
                 )
-                h_code_tiles[r] = (h_codes, h_scales)
+                h_code_tiles[pair] = (h_codes, h_scales)
 
-            def project(r, t):
-                j, i = place_of(r, t)
-                h_codes, h_scales = h_code_tiles[r]
+            def project(q):
+                pair, t = divmod(q, PAIR)
+                h_codes, h_scales = h_code_tiles[pair]
                 columns = slice(t * P, (t + 1) * P)
-                o_sb = o_pool.tile([P, D_MODEL], F32, name="o_sb")
-                first_ps = mm_psum.tile([P, BANK], F32, name="first_ps", tag="mm")
-                second_ps = mm_psum.tile([P, BANK], F32, name="second_ps", tag="mm")
-                first_half, second_half = slice(0, BANK), slice(BANK, 2 * BANK)
-                for o_ps, half in ((first_ps, first_half), (second_ps, second_half), (first_ps, first_half)):
+                for n in range(OUT_HALVES):
+                    half = slice(n * BANK, (n + 1) * BANK)
+                    o_ps = mm_psum.tile([P, BANK], F32, name="o_ps", tag="mm")
                     nc.tensor.matmul_mx(
                         out=o_ps[:],
                         lhsT=h_codes[:, columns].bitcast(FP8X4),
@@ -292,28 +289,32 @@ def tile_gatedmultiscaleretentionlayer_pc_t_kernel(tc, x, ret, Wg, bg, Wo, bo, o
                         start=True,
                         stop=True,
                     )
-                nc.scalar.copy(out=o_sb[:, second_half], in_=second_ps[:])
+                    o_banks[q, n] = o_ps
+
+            def add_bias_and_store(q):
+                j, i = divmod(q, TILES)
+                first_half, second_half = slice(0, BANK), slice(BANK, 2 * BANK)
+                o_sb = o_pool.tile([P, D_MODEL], F32, name="o_sb")
+                nc.vector.tensor_tensor(
+                    out=o_sb[:, first_half], in0=o_banks[q, 0][:], in1=bo_all[:, first_half], op=ALU.add
+                )
+                nc.scalar.copy(out=o_sb[:, second_half], in_=o_banks[q, 1][:])
                 nc.gpsimd.tensor_tensor(
                     out=o_sb[:, second_half], in0=o_sb[:, second_half], in1=bo_all[:, second_half], op=ALU.add
                 )
-                nc.vector.tensor_tensor(out=o_sb[:, first_half], in0=first_ps[:], in1=bo_all[:, first_half], op=ALU.add)
                 group_rows = out_rows[j * GROUP : (j + 1) * GROUP, :].rearrange("(p i) n -> p i n", i=TILES)
                 nc.sync.dma_start(out=group_rows[:, i, :], in_=o_sb[:])
 
-            for t in range(PAIR):
-                normalise(0, t)
-            for t in range(PAIR):
-                normalise(1, t)
-                transpose_gn(0, t)
-                multiply(0, t)
-            quantise_h(0)
-            for r in range(N_PAIRS):
-                for t in range(PAIR):
-                    if r + 2 < N_PAIRS:
-                        normalise(r + 2, t)
-                    if r + 1 < N_PAIRS:
-                        transpose_gn(r + 1, t)
-                        multiply(r + 1, t)
-                    project(r, t)
-                if r + 1 < N_PAIRS:
-                    quantise_h(r + 1)
+            for step in range(-NORMALISE_AHEAD, N_TILES):
+                if 0 <= step + NORMALISE_AHEAD < N_TILES:
+                    normalise(step + NORMALISE_AHEAD)
+                if 0 <= step + TRANSPOSE_AHEAD < N_TILES:
+                    transpose_gn(step + TRANSPOSE_AHEAD)
+                if 0 <= step + MULTIPLY_AHEAD < N_TILES:
+                    multiply(step + MULTIPLY_AHEAD)
+                if 0 <= step + PROJECT_AHEAD < N_TILES:
+                    project(step + PROJECT_AHEAD)
+                if 0 <= step:
+                    add_bias_and_store(step)
+                if 0 <= step + MULTIPLY_AHEAD < N_TILES and (step + MULTIPLY_AHEAD) % PAIR == PAIR - 1:
+                    quantise_h((step + MULTIPLY_AHEAD) // PAIR)

@@ -30,9 +30,12 @@ NORMS = HEADS * TILES
 STATS = 6
 QUARTER = D_HEAD // PACK
 PAIR = 2
-N_TILES = BATCH * SEQ // P
-NORMALISE_AHEAD, TRANSPOSE_AHEAD, MULTIPLY_AHEAD, PROJECT_AHEAD = 7, 5, 4, 1
 PAIRS_PER_GROUP = TILES // PAIR
+N_TILES = BATCH * SEQ // P
+N_X_PASSES = N_GROUPS * X_PASSES
+HEADS_PER_STEP = HEADS // X_PASSES
+TRANSPOSE_X_AHEAD, EMPTY_X_AHEAD, QUANTISE_X_AHEAD, LOAD_GROUPS_AHEAD = 4, 3, 2, 4
+NORMALISE_AHEAD, TRANSPOSE_AHEAD, MULTIPLY_AHEAD, PROJECT_AHEAD = 9, 7, 6, 1
 FEATURE_TILES_PER_RUN = PACK // X_PASSES
 WO_SLICE = D_MODEL // N_GROUPS
 
@@ -47,7 +50,7 @@ def tile_gatedmultiscaleretentionlayer_pc_t_kernel(tc, x, ret, Wg, bg, Wo, bo, o
     with ExitStack() as whole:
         whole.enter_context(tc.manual_schedule())
         const = whole.enter_context(tc.tile_pool(name="const", bufs=1))
-        stat_pool = whole.enter_context(tc.tile_pool(name="stat", bufs=2))
+        stat_pool = whole.enter_context(tc.tile_pool(name="stat", bufs=3))
         tp_psum = whole.enter_context(tc.psum_pool(name="tp", bufs=4))
         mm_psum = whole.enter_context(tc.psum_pool(name="mm", bufs=4))
 
@@ -66,15 +69,16 @@ def tile_gatedmultiscaleretentionlayer_pc_t_kernel(tc, x, ret, Wg, bg, Wo, bo, o
         bo_all = const.tile([P, D_MODEL], BF16, name="bo_all")
         ret_all = const.tile([P, N_GROUPS, HEADS, TILES, D_HEAD], BF16, name="ret_all")
         gate_all = const.tile([P, N_GROUPS, PACK, GROUP], F32, name="gate_all")
+        mean_var = const.tile([P, N_GROUPS, NORMS, 2], F32, name="mean_var")
         rstd = const.tile([P, N_GROUPS, NORMS], F32, name="rstd")
         shift = const.tile([P, N_GROUPS, NORMS], F32, name="shift")
 
         with ExitStack() as part_one:
             w_pool = part_one.enter_context(tc.tile_pool(name="w", bufs=1))
-            x_pool = part_one.enter_context(tc.tile_pool(name="x", bufs=3))
-            xq_pool = part_one.enter_context(tc.tile_pool(name="xq", bufs=2 * X_PASSES))
+            x_pool = part_one.enter_context(tc.tile_pool(name="x", bufs=LOAD_GROUPS_AHEAD))
+            xq_pool = part_one.enter_context(tc.tile_pool(name="xq", bufs=4))
 
-            x_tiles, x_grouped_tiles, x_code_tiles = {}, {}, {}
+            x_tiles, xT_tiles, x_grouped_tiles, x_code_tiles = {}, {}, {}, {}
 
             def load_group(j):
                 rows = slice(j * GROUP, (j + 1) * GROUP)
@@ -88,10 +92,9 @@ def tile_gatedmultiscaleretentionlayer_pc_t_kernel(tc, x, ret, Wg, bg, Wo, bo, o
                 )
                 x_tiles[j] = x_sb
 
-            def transpose_x(j, g):
+            def transpose_x(k):
+                j, g = divmod(k, X_PASSES)
                 x_words = x_tiles[j][:].bitcast(F32)
-                x_grouped = xq_pool.tile([P, GROUP, PACK], BF16, name="x_grouped", align_bytes=64)
-                x_grouped_words = x_grouped[:].bitcast(F32)
                 for pair in range(PAIRS_PER_GROUP):
                     xT = tp_psum.tile([P, 2, PAIR * P], F32, name="xT", tag="tp")
                     for r in range(PAIR):
@@ -102,27 +105,33 @@ def tile_gatedmultiscaleretentionlayer_pc_t_kernel(tc, x, ret, Wg, bg, Wo, bo, o
                                 in_=x_words[:, PAIR * pair + r, first : first + P],
                                 identity=ident[:],
                             )
+                    xT_tiles[k, pair] = xT
+
+            def empty_x(k):
+                x_grouped = xq_pool.tile([P, GROUP, PACK], BF16, name="x_grouped", align_bytes=64)
+                x_grouped_words = x_grouped[:].bitcast(F32)
+                for pair in range(PAIRS_PER_GROUP):
                     nc.scalar.copy(
                         out=x_grouped_words[:, pair * PAIR * P : (pair + 1) * PAIR * P, :],
-                        in_=xT[:].rearrange("p u s -> p s u"),
+                        in_=xT_tiles[k, pair][:].rearrange("p u s -> p s u"),
                     )
-                x_grouped_tiles[j, g] = x_grouped
+                x_grouped_tiles[k] = x_grouped
 
-            def quantise_x(j, g):
+            def quantise_x(k):
                 x_codes = xq_pool.tile([P, GROUP], U32, name="x_codes", align_bytes=64)
                 x_scales = xq_pool.tile([P, GROUP], U8, name="x_scales", align_bytes=64)
                 nc.vector.quantize_mx(
                     out=x_codes[:].bitcast(FP8X4),
                     scales=x_scales[:],
-                    in_=x_grouped_tiles[j, g][:].rearrange("p s k -> p (s k)"),
+                    in_=x_grouped_tiles[k][:].rearrange("p s k -> p (s k)"),
                 )
-                x_code_tiles[j, g] = (x_codes, x_scales)
+                x_code_tiles[k] = (x_codes, x_scales)
 
             def gate_features(j, f):
                 features = slice(f * P, (f + 1) * P)
                 z = mm_psum.tile([P, GROUP], F32, name="z", tag="mm")
                 for g in range(X_PASSES):
-                    x_codes, x_scales = x_code_tiles[j, g]
+                    x_codes, x_scales = x_code_tiles[j * X_PASSES + g]
                     nc.tensor.matmul_mx(
                         out=z[:],
                         lhsT=wg_codes[:, g, features].bitcast(FP8X4),
@@ -136,31 +145,22 @@ def tile_gatedmultiscaleretentionlayer_pc_t_kernel(tc, x, ret, Wg, bg, Wo, bo, o
                     out=gate_all[:, j, f, :], in_=z[:], func=ACT.Silu, bias=bg_col[:, f : f + 1], scale=1.0
                 )
 
-            def norm_stage(j):
-                stats = stat_pool.tile([P, NORMS, STATS], F32, name="stats")
-                for h in range(HEADS):
-                    for i in range(TILES):
-                        nc.vector.bn_stats(out=stats[:, h * TILES + i, :], in_=ret_all[:, j, h, i, :])
-                mean_e, ssd_e, mean_o, ssd_o = stats[:, :, 1], stats[:, :, 2], stats[:, :, 4], stats[:, :, 5]
-                mean_sum = stat_pool.tile([P, NORMS], F32, name="mean_sum")
-                nc.vector.tensor_tensor(out=mean_sum[:], in0=mean_e, in1=mean_o, op=ALU.add)
-                mean_gap = stat_pool.tile([P, NORMS], F32, name="mean_gap")
-                nc.vector.tensor_tensor(out=mean_gap[:], in0=mean_e, in1=mean_o, op=ALU.subtract)
-                ssd_halves = stat_pool.tile([P, NORMS], F32, name="ssd_halves")
-                nc.vector.tensor_tensor(out=ssd_halves[:], in0=ssd_e, in1=ssd_o, op=ALU.add)
-                gap_sq = stat_pool.tile([P, NORMS], F32, name="gap_sq")
-                nc.vector.tensor_tensor(out=gap_sq[:], in0=mean_gap[:], in1=mean_gap[:], op=ALU.mult)
-                ssd = stat_pool.tile([P, NORMS], F32, name="ssd")
-                nc.vector.scalar_tensor_tensor(
-                    out=ssd[:], in0=gap_sq[:], scalar=D_HEAD / 4.0, in1=ssd_halves[:], op0=ALU.mult, op1=ALU.add
-                )
+            def norm_stats(j, heads):
+                stats = stat_pool.tile([P, HEADS_PER_STEP * TILES, STATS], F32, name="stats")
+                norms = [(h, i) for h in heads for i in range(TILES)]
+                for n, (h, i) in enumerate(norms):
+                    nc.vector.bn_stats(out=stats[:, n, :], in_=ret_all[:, j, h, i, :])
+                for n, (h, i) in enumerate(norms):
+                    nc.vector.bn_aggr(out=mean_var[:, j, h * TILES + i, :], in_=stats[:, n, :])
+
+            def norm_scale_shift(j):
                 var_eps = stat_pool.tile([P, NORMS], F32, name="var_eps")
                 nc.gpsimd.tensor_scalar(
-                    out=var_eps[:], in0=ssd[:], scalar1=1.0 / D_HEAD, scalar2=EPS, op0=ALU.mult, op1=ALU.add
+                    out=var_eps[:], in0=mean_var[:, j, :, 1], scalar1=1.0, scalar2=EPS, op0=ALU.mult, op1=ALU.add
                 )
                 minus_mean = stat_pool.tile([P, NORMS], F32, name="minus_mean")
                 nc.gpsimd.tensor_scalar(
-                    out=minus_mean[:], in0=mean_sum[:], scalar1=-0.5, scalar2=0.0, op0=ALU.mult, op1=ALU.add
+                    out=minus_mean[:], in0=mean_var[:, j, :, 0], scalar1=-1.0, scalar2=0.0, op0=ALU.mult, op1=ALU.add
                 )
                 nc.gpsimd.tensor_tensor(out=rstd[:, j, :], in0=var_eps[:], in1=minus_half[:], op=ALU.pow)
                 nc.gpsimd.tensor_tensor(out=shift[:, j, :], in0=minus_mean[:], in1=rstd[:, j, :], op=ALU.mult)
@@ -190,7 +190,6 @@ def tile_gatedmultiscaleretentionlayer_pc_t_kernel(tc, x, ret, Wg, bg, Wo, bo, o
             load_group(1)
             wo_raw = w_pool.tile([P, PACK, D_MODEL], BF16, name="wo_raw")
             nc.sync.dma_start(out=wo_raw[:], in_=Wo.rearrange("(p k) n -> p k n", k=PACK))
-            nc.sync.dma_start(out=bo_all[:], in_=bo.partition_broadcast(P))
 
             wg_grouped = w_pool.tile([P, X_PASSES, PACK, P, PACK], BF16, name="wg_grouped", align_bytes=64)
             wo_grouped = w_pool.tile([P, D_MODEL, PACK], BF16, name="wo_grouped", align_bytes=64)
@@ -206,27 +205,30 @@ def tile_gatedmultiscaleretentionlayer_pc_t_kernel(tc, x, ret, Wg, bg, Wo, bo, o
                 )
             nc.vector.tensor_copy(out=bg_col[:], in_=bg_bf[:])
 
-            for g in range(X_PASSES):
-                transpose_x(0, g)
-                quantise_x(0, g)
-            for j in range(N_GROUPS):
-                if j + 2 < N_GROUPS:
-                    load_group(j + 2)
-                for g in range(X_PASSES):
-                    if j + 1 < N_GROUPS:
-                        transpose_x(j + 1, g)
+            for k in range(-TRANSPOSE_X_AHEAD, N_X_PASSES):
+                j, g = divmod(k, X_PASSES)
+                if g == 0 and j + LOAD_GROUPS_AHEAD < N_GROUPS:
+                    load_group(j + LOAD_GROUPS_AHEAD)
+                if k + TRANSPOSE_X_AHEAD < N_X_PASSES:
+                    transpose_x(k + TRANSPOSE_X_AHEAD)
+                if 0 <= k + EMPTY_X_AHEAD < N_X_PASSES:
+                    empty_x(k + EMPTY_X_AHEAD)
+                if 0 <= k + QUANTISE_X_AHEAD < N_X_PASSES:
+                    quantise_x(k + QUANTISE_X_AHEAD)
+                if 0 <= k:
                     for f in range(g * FEATURE_TILES_PER_RUN, (g + 1) * FEATURE_TILES_PER_RUN):
                         gate_features(j, f)
-                norm_stage(j)
-                regroup_wo_slice(j)
-                if j + 1 < N_GROUPS:
-                    for g in range(X_PASSES):
-                        quantise_x(j + 1, g)
-                quantise_wo_slice(j)
+                    norm_stats(j, range(g * HEADS_PER_STEP, (g + 1) * HEADS_PER_STEP))
+                    if g == 0:
+                        regroup_wo_slice(j)
+                    if g == X_PASSES - 1:
+                        quantise_wo_slice(j)
+                        norm_scale_shift(j)
+            nc.sync.dma_start(out=bo_all[:], in_=bo.partition_broadcast(P))
 
         with ExitStack() as part_two:
             gn_pool = part_two.enter_context(tc.tile_pool(name="gn", bufs=4))
-            hq_pool = part_two.enter_context(tc.tile_pool(name="hq", bufs=3))
+            hq_pool = part_two.enter_context(tc.tile_pool(name="hq", bufs=2))
             o_pool = part_two.enter_context(tc.tile_pool(name="o", bufs=8))
 
             gn_tiles, gnT_tiles, h_grouped_tiles, h_code_tiles, o_banks = {}, {}, {}, {}, {}
@@ -253,30 +255,30 @@ def tile_gatedmultiscaleretentionlayer_pc_t_kernel(tc, x, ret, Wg, bg, Wo, bo, o
 
             def multiply(q):
                 j, i = divmod(q, TILES)
-                pair, t = divmod(q, PAIR)
-                if t == 0:
-                    h_grouped_tiles[pair] = hq_pool.tile([P, PAIR * P, PACK], BF16, name="h_grouped", align_bytes=64)
+                columns = slice(i * P, (i + 1) * P)
+                if i == 0:
+                    h_grouped_tiles[j] = hq_pool.tile([P, GROUP, PACK], BF16, name="h_grouped", align_bytes=64)
                 nc.vector.tensor_tensor(
-                    out=h_grouped_tiles[pair][:, t * P : (t + 1) * P, :],
+                    out=h_grouped_tiles[j][:, columns, :],
                     in0=gnT_tiles[q][:].rearrange("p f s -> p s f"),
-                    in1=gate_all[:, j, :, i * P : (i + 1) * P].rearrange("p f s -> p s f"),
+                    in1=gate_all[:, j, :, columns].rearrange("p f s -> p s f"),
                     op=ALU.mult,
                 )
 
-            def quantise_h(pair):
-                h_codes = hq_pool.tile([P, PAIR * P], U32, name="h_codes", align_bytes=64)
-                h_scales = hq_pool.tile([P, PAIR * P], U8, name="h_scales", align_bytes=64)
+            def quantise_h(j):
+                h_codes = hq_pool.tile([P, GROUP], U32, name="h_codes", align_bytes=64)
+                h_scales = hq_pool.tile([P, GROUP], U8, name="h_scales", align_bytes=64)
                 nc.vector.quantize_mx(
                     out=h_codes[:].bitcast(FP8X4),
                     scales=h_scales[:],
-                    in_=h_grouped_tiles[pair][:].rearrange("p s k -> p (s k)"),
+                    in_=h_grouped_tiles[j][:].rearrange("p s k -> p (s k)"),
                 )
-                h_code_tiles[pair] = (h_codes, h_scales)
+                h_code_tiles[j] = (h_codes, h_scales)
 
             def project(q):
-                pair, t = divmod(q, PAIR)
-                h_codes, h_scales = h_code_tiles[pair]
-                columns = slice(t * P, (t + 1) * P)
+                j, i = divmod(q, TILES)
+                h_codes, h_scales = h_code_tiles[j]
+                columns = slice(i * P, (i + 1) * P)
                 for n in range(OUT_HALVES):
                     half = slice(n * BANK, (n + 1) * BANK)
                     o_ps = mm_psum.tile([P, BANK], F32, name="o_ps", tag="mm")
@@ -316,5 +318,5 @@ def tile_gatedmultiscaleretentionlayer_pc_t_kernel(tc, x, ret, Wg, bg, Wo, bo, o
                     project(step + PROJECT_AHEAD)
                 if 0 <= step:
                     add_bias_and_store(step)
-                if 0 <= step + MULTIPLY_AHEAD < N_TILES and (step + MULTIPLY_AHEAD) % PAIR == PAIR - 1:
-                    quantise_h((step + MULTIPLY_AHEAD) // PAIR)
+                if 0 <= step + MULTIPLY_AHEAD < N_TILES and (step + MULTIPLY_AHEAD) % TILES == TILES - 1:
+                    quantise_h((step + MULTIPLY_AHEAD) // TILES)

@@ -36,6 +36,7 @@ N_X_PASSES = N_GROUPS * X_PASSES
 HEADS_PER_STEP = HEADS // X_PASSES
 TRANSPOSE_X_AHEAD, EMPTY_X_AHEAD, QUANTISE_X_AHEAD, LOAD_GROUPS_AHEAD = 4, 3, 2, 4
 NORMALISE_AHEAD, TRANSPOSE_AHEAD, MULTIPLY_AHEAD, PROJECT_AHEAD = 9, 7, 6, 1
+VECTOR_ALONE_EVERY = 4
 FEATURE_TILES_PER_RUN = PACK // X_PASSES
 WO_SLICE = D_MODEL // N_GROUPS
 
@@ -300,10 +301,15 @@ def tile_gatedmultiscaleretentionlayer_pc_t_kernel(tc, x, ret, Wg, bg, Wo, bo, o
                 nc.vector.tensor_tensor(
                     out=o_sb[:, first_half], in0=o_banks[q, 0][:], in1=bo_all[:, first_half], op=ALU.add
                 )
-                nc.scalar.copy(out=o_sb[:, second_half], in_=o_banks[q, 1][:])
-                nc.gpsimd.tensor_tensor(
-                    out=o_sb[:, second_half], in0=o_sb[:, second_half], in1=bo_all[:, second_half], op=ALU.add
-                )
+                if q % VECTOR_ALONE_EVERY == VECTOR_ALONE_EVERY - 1:
+                    nc.vector.tensor_tensor(
+                        out=o_sb[:, second_half], in0=o_banks[q, 1][:], in1=bo_all[:, second_half], op=ALU.add
+                    )
+                else:
+                    nc.scalar.copy(out=o_sb[:, second_half], in_=o_banks[q, 1][:])
+                    nc.gpsimd.tensor_tensor(
+                        out=o_sb[:, second_half], in0=o_sb[:, second_half], in1=bo_all[:, second_half], op=ALU.add
+                    )
                 group_rows = out_rows[j * GROUP : (j + 1) * GROUP, :].rearrange("(p i) n -> p i n", i=TILES)
                 nc.sync.dma_start(out=group_rows[:, i, :], in_=o_sb[:])
 

from contextlib import ExitStack

import concourse.mybir as mybir
from concourse.masks import make_identity

F32 = mybir.dt.float32
BF16 = mybir.dt.bfloat16
U32 = mybir.dt.uint32
U8 = mybir.dt.uint8
FP8X4 = mybir.dt.float8_e4m3fn_x4
ALU = mybir.AluOpType
ACT = mybir.ActivationFunctionType

P = 128
PACK = 4
K_PASS = P * PACK
BANK = 512

BATCH, SEQ, D_MODEL, HEADS, D_HEAD = 4, 1024, 1024, 4, 128
D_INNER = HEADS * D_HEAD
EPS = 1e-5

GROUP = 512
TILES = GROUP // P
N_GROUPS = BATCH * SEQ // GROUP
GROUPS_PER_BATCH = SEQ // GROUP
X_PASSES = D_MODEL // K_PASS
OUT_HALVES = D_MODEL // BANK
NORMS = HEADS * TILES
STATS = 6
QUARTER = D_HEAD // PACK
PAIR = 2
PAIRS_PER_GROUP = TILES // PAIR
N_TILES = BATCH * SEQ // P
N_X_PASSES = N_GROUPS * X_PASSES
HEADS_PER_STEP = HEADS // X_PASSES
TRANSPOSE_X_AHEAD, EMPTY_X_AHEAD, QUANTISE_X_AHEAD, LOAD_GROUPS_AHEAD = 4, 3, 2, 4
NORMALISE_AHEAD, TRANSPOSE_AHEAD, MULTIPLY_AHEAD, PROJECT_AHEAD = 9, 7, 6, 1
VECTOR_ALONE_EVERY = 4
FEATURE_TILES_PER_RUN = PACK // X_PASSES
WO_SLICE = D_MODEL // N_GROUPS

FLOPS = 2 * BATCH * SEQ * (D_MODEL * D_INNER + D_INNER * D_MODEL)


def tile_gatedmultiscaleretentionlayer_pc_t_kernel(tc, x, ret, Wg, bg, Wo, bo, out):
    nc = tc.nc
    x_rows = x.flatten_outer_dims()
    out_rows = out.flatten_outer_dims()

    with ExitStack() as whole:
        whole.enter_context(tc.manual_schedule())
        const = whole.enter_context(tc.tile_pool(name="const", bufs=1))
        stat_pool = whole.enter_context(tc.tile_pool(name="stat", bufs=3))
        tp_psum = whole.enter_context(tc.psum_pool(name="tp", bufs=4))
        mm_psum = whole.enter_context(tc.psum_pool(name="mm", bufs=4))

        ident = const.tile([P, P], F32, name="ident")
        make_identity(nc, ident[:])
        minus_half = const.tile([P, NORMS], F32, name="minus_half")
        nc.gpsimd.memset(minus_half[:], -0.5)
        table_warmer = const.tile([P, 1], F32, name="table_warmer")
        nc.scalar.activation(out=table_warmer[:], in_=minus_half[:, 0:1], func=ACT.Silu)

        wg_codes = const.tile([P, X_PASSES, D_INNER], U32, name="wg_codes", align_bytes=64)
        wg_scales = const.tile([P, X_PASSES, D_INNER], U8, name="wg_scales", align_bytes=64)
        wo_codes = const.tile([P, D_MODEL], U32, name="wo_codes", align_bytes=64)
        wo_scales = const.tile([P, D_MODEL], U8, name="wo_scales", align_bytes=64)
        bg_col = const.tile([P, PACK], F32, name="bg_col")
        bo_all = const.tile([P, D_MODEL], BF16, name="bo_all")
        ret_all = const.tile([P, N_GROUPS, HEADS, TILES, D_HEAD], BF16, name="ret_all")
        gate_all = const.tile([P, N_GROUPS, PACK, GROUP], F32, name="gate_all")
        mean_var = const.tile([P, N_GROUPS, NORMS, 2], F32, name="mean_var")
        rstd = const.tile([P, N_GROUPS, NORMS], F32, name="rstd")
        shift = const.tile([P, N_GROUPS, NORMS], F32, name="shift")

        with ExitStack() as part_one:
            w_pool = part_one.enter_context(tc.tile_pool(name="w", bufs=1))
            x_pool = part_one.enter_context(tc.tile_pool(name="x", bufs=LOAD_GROUPS_AHEAD))
            xq_pool = part_one.enter_context(tc.tile_pool(name="xq", bufs=4))

            x_tiles, xT_tiles, x_grouped_tiles, x_code_tiles = {}, {}, {}, {}

            def load_group(j):
                rows = slice(j * GROUP, (j + 1) * GROUP)
                x_sb = x_pool.tile([P, TILES, D_MODEL], BF16, name="x_sb")
                nc.sync.dma_start(out=x_sb[:], in_=x_rows[rows, :].rearrange("(p i) k -> p i k", i=TILES))
                b, part = divmod(j, GROUPS_PER_BATCH)
                positions = slice(part * GROUP, (part + 1) * GROUP)
                nc.sync.dma_start(
                    out=ret_all[:, j, :, :, :].rearrange("p h i d -> p h (i d)"),
                    in_=ret[b, :, positions, :].rearrange("h (p i) d -> p h (i d)", i=TILES),
                )
                x_tiles[j] = x_sb

            def transpose_x(k):
                j, g = divmod(k, X_PASSES)
                x_words = x_tiles[j][:].bitcast(F32)
                for pair in range(PAIRS_PER_GROUP):
                    xT = tp_psum.tile([P, 2, PAIR * P], F32, name="xT", tag="tp")
                    for r in range(PAIR):
                        for u in range(2):
                            first = (2 * g + u) * P
                            nc.tensor.transpose(
                                out=xT[:, u, r * P : (r + 1) * P],
                                in_=x_words[:, PAIR * pair + r, first : first + P],
                                identity=ident[:],
                            )
                    xT_tiles[k, pair] = xT

            def empty_x(k):
                x_grouped = xq_pool.tile([P, GROUP, PACK], BF16, name="x_grouped", align_bytes=64)
                x_grouped_words = x_grouped[:].bitcast(F32)
                for pair in range(PAIRS_PER_GROUP):
                    nc.scalar.copy(
                        out=x_grouped_words[:, pair * PAIR * P : (pair + 1) * PAIR * P, :],
                        in_=xT_tiles[k, pair][:].rearrange("p u s -> p s u"),
                    )
                x_grouped_tiles[k] = x_grouped

            def quantise_x(k):
                x_codes = xq_pool.tile([P, GROUP], U32, name="x_codes", align_bytes=64)
                x_scales = xq_pool.tile([P, GROUP], U8, name="x_scales", align_bytes=64)
                nc.vector.quantize_mx(
                    out=x_codes[:].bitcast(FP8X4),
                    scales=x_scales[:],
                    in_=x_grouped_tiles[k][:].rearrange("p s k -> p (s k)"),
                )
                x_code_tiles[k] = (x_codes, x_scales)

            def gate_features(j, f):
                features = slice(f * P, (f + 1) * P)
                z = mm_psum.tile([P, GROUP], F32, name="z", tag="mm")
                for g in range(X_PASSES):
                    x_codes, x_scales = x_code_tiles[j * X_PASSES + g]
                    nc.tensor.matmul_mx(
                        out=z[:],
                        lhsT=wg_codes[:, g, features].bitcast(FP8X4),
                        lhsT_scale=wg_scales[:, g, features],
                        rhs=x_codes[:].bitcast(FP8X4),
                        rhs_scale=x_scales[:],
                        start=(g == 0),
                        stop=(g == X_PASSES - 1),
                    )
                nc.scalar.activation(
                    out=gate_all[:, j, f, :], in_=z[:], func=ACT.Silu, bias=bg_col[:, f : f + 1], scale=1.0
                )

            def norm_stats(j, heads):
                stats = stat_pool.tile([P, HEADS_PER_STEP * TILES, STATS], F32, name="stats")
                norms = [(h, i) for h in heads for i in range(TILES)]
                for n, (h, i) in enumerate(norms):
                    nc.vector.bn_stats(out=stats[:, n, :], in_=ret_all[:, j, h, i, :])
                for n, (h, i) in enumerate(norms):
                    nc.vector.bn_aggr(out=mean_var[:, j, h * TILES + i, :], in_=stats[:, n, :])

            def norm_scale_shift(j):
                var_eps = stat_pool.tile([P, NORMS], F32, name="var_eps")
                nc.gpsimd.tensor_scalar(
                    out=var_eps[:], in0=mean_var[:, j, :, 1], scalar1=1.0, scalar2=EPS, op0=ALU.mult, op1=ALU.add
                )
                minus_mean = stat_pool.tile([P, NORMS], F32, name="minus_mean")
                nc.gpsimd.tensor_scalar(
                    out=minus_mean[:], in0=mean_var[:, j, :, 0], scalar1=-1.0, scalar2=0.0, op0=ALU.mult, op1=ALU.add
                )
                nc.gpsimd.tensor_tensor(out=rstd[:, j, :], in0=var_eps[:], in1=minus_half[:], op=ALU.pow)
                nc.gpsimd.tensor_tensor(out=shift[:, j, :], in0=minus_mean[:], in1=rstd[:, j, :], op=ALU.mult)

            def regroup_wo_slice(j):
                columns = slice(j * WO_SLICE, (j + 1) * WO_SLICE)
                nc.vector.tensor_copy(
                    out=wo_grouped[:, columns, :], in_=wo_raw[:, :, columns].rearrange("p k n -> p n k")
                )

            def quantise_wo_slice(j):
                columns = slice(j * WO_SLICE, (j + 1) * WO_SLICE)
                nc.vector.quantize_mx(
                    out=wo_codes[:, columns].bitcast(FP8X4),
                    scales=wo_scales[:, columns],
                    in_=wo_grouped[:, columns, :].rearrange("p n k -> p (n k)"),
                )

            wg_raw = w_pool.tile([P, X_PASSES, PACK, D_INNER], BF16, name="wg_raw")
            nc.sync.dma_start(
                out=wg_raw[:].rearrange("p g (u e) c -> p (g u) (e c)", e=2),
                in_=Wg.rearrange("(g u p e) c -> p (g u) (e c)", g=X_PASSES, u=2, e=2),
            )
            load_group(0)
            bg_bf = w_pool.tile([P, PACK], BF16, name="bg_bf")
            nc.sync.dma_start(out=bg_bf[:], in_=bg.rearrange("(m f) -> m f", f=PACK))
            load_group(1)
            wo_raw = w_pool.tile([P, PACK, D_MODEL], BF16, name="wo_raw")
            nc.sync.dma_start(out=wo_raw[:], in_=Wo.rearrange("(p k) n -> p k n", k=PACK))

            wg_grouped = w_pool.tile([P, X_PASSES, PACK, P, PACK], BF16, name="wg_grouped", align_bytes=64)
            wo_grouped = w_pool.tile([P, D_MODEL, PACK], BF16, name="wo_grouped", align_bytes=64)
            for g in range(X_PASSES):
                nc.vector.tensor_copy(
                    out=wg_grouped[:, g, :, :, :], in_=wg_raw[:, g, :, :].rearrange("p k (m f) -> p f m k", f=PACK)
                )
            for g in range(X_PASSES):
                nc.vector.quantize_mx(
                    out=wg_codes[:, g, :].bitcast(FP8X4),
                    scales=wg_scales[:, g, :],
                    in_=wg_grouped[:, g, :, :, :].rearrange("p f m k -> p (f m k)"),
                )
            nc.vector.tensor_copy(out=bg_col[:], in_=bg_bf[:])

            for k in range(-TRANSPOSE_X_AHEAD, N_X_PASSES):
                j, g = divmod(k, X_PASSES)
                if g == 0 and j + LOAD_GROUPS_AHEAD < N_GROUPS:
                    load_group(j + LOAD_GROUPS_AHEAD)
                if k + TRANSPOSE_X_AHEAD < N_X_PASSES:
                    transpose_x(k + TRANSPOSE_X_AHEAD)
                if 0 <= k + EMPTY_X_AHEAD < N_X_PASSES:
                    empty_x(k + EMPTY_X_AHEAD)
                if 0 <= k + QUANTISE_X_AHEAD < N_X_PASSES:
                    quantise_x(k + QUANTISE_X_AHEAD)
                if 0 <= k:
                    for f in range(g * FEATURE_TILES_PER_RUN, (g + 1) * FEATURE_TILES_PER_RUN):
                        gate_features(j, f)
                    norm_stats(j, range(g * HEADS_PER_STEP, (g + 1) * HEADS_PER_STEP))
                    if g == 0:
                        regroup_wo_slice(j)
                    if g == X_PASSES - 1:
                        quantise_wo_slice(j)
                        norm_scale_shift(j)
            nc.sync.dma_start(out=bo_all[:], in_=bo.partition_broadcast(P))

        with ExitStack() as part_two:
            gn_pool = part_two.enter_context(tc.tile_pool(name="gn", bufs=4))
            hq_pool = part_two.enter_context(tc.tile_pool(name="hq", bufs=2))
            o_pool = part_two.enter_context(tc.tile_pool(name="o", bufs=8))

            gn_tiles, gnT_tiles, h_grouped_tiles, h_code_tiles, o_banks = {}, {}, {}, {}, {}

            def normalise(q):
                j, i = divmod(q, TILES)
                gn = gn_pool.tile([P, PACK, P], F32, name="gn")
                for h in range(HEADS):
                    norm = h * TILES + i
                    nc.scalar.activation(
                        out=gn[:, :, h * QUARTER : (h + 1) * QUARTER],
                        in_=ret_all[:, j, h, i, :].rearrange("p (m f) -> p f m", f=PACK),
                        func=ACT.Identity,
                        scale=rstd[:, j, norm : norm + 1],
                        bias=shift[:, j, norm : norm + 1],
                    )
                gn_tiles[q] = gn

            def transpose_gn(q):
                gnT = tp_psum.tile([P, PACK, P], F32, name="gnT", tag="tp")
                for f in range(PACK):
                    nc.tensor.transpose(out=gnT[:, f, :], in_=gn_tiles[q][:, f, :], identity=ident[:])
                gnT_tiles[q] = gnT

            def multiply(q):
                j, i = divmod(q, TILES)
                columns = slice(i * P, (i + 1) * P)
                if i == 0:
                    h_grouped_tiles[j] = hq_pool.tile([P, GROUP, PACK], BF16, name="h_grouped", align_bytes=64)
                nc.vector.tensor_tensor(
                    out=h_grouped_tiles[j][:, columns, :],
                    in0=gnT_tiles[q][:].rearrange("p f s -> p s f"),
                    in1=gate_all[:, j, :, columns].rearrange("p f s -> p s f"),
                    op=ALU.mult,
                )

            def quantise_h(j):
                h_codes = hq_pool.tile([P, GROUP], U32, name="h_codes", align_bytes=64)
                h_scales = hq_pool.tile([P, GROUP], U8, name="h_scales", align_bytes=64)
                nc.vector.quantize_mx(
                    out=h_codes[:].bitcast(FP8X4),
                    scales=h_scales[:],
                    in_=h_grouped_tiles[j][:].rearrange("p s k -> p (s k)"),
                )
                h_code_tiles[j] = (h_codes, h_scales)

            def project(q):
                j, i = divmod(q, TILES)
                h_codes, h_scales = h_code_tiles[j]
                columns = slice(i * P, (i + 1) * P)
                for n in range(OUT_HALVES):
                    half = slice(n * BANK, (n + 1) * BANK)
                    o_ps = mm_psum.tile([P, BANK], F32, name="o_ps", tag="mm")
                    nc.tensor.matmul_mx(
                        out=o_ps[:],
                        lhsT=h_codes[:, columns].bitcast(FP8X4),
                        lhsT_scale=h_scales[:, columns],
                        rhs=wo_codes[:, half].bitcast(FP8X4),
                        rhs_scale=wo_scales[:, half],
                        start=True,
                        stop=True,
                    )
                    o_banks[q, n] = o_ps

            def add_bias_and_store(q):
                j, i = divmod(q, TILES)
                first_half, second_half = slice(0, BANK), slice(BANK, 2 * BANK)
                o_sb = o_pool.tile([P, D_MODEL], F32, name="o_sb")
                nc.vector.tensor_tensor(
                    out=o_sb[:, first_half], in0=o_banks[q, 0][:], in1=bo_all[:, first_half], op=ALU.add
                )
                if q % VECTOR_ALONE_EVERY == VECTOR_ALONE_EVERY - 1:
                    nc.vector.tensor_tensor(
                        out=o_sb[:, second_half], in0=o_banks[q, 1][:], in1=bo_all[:, second_half], op=ALU.add
                    )
                else:
                    nc.scalar.copy(out=o_sb[:, second_half], in_=o_banks[q, 1][:])
                    nc.gpsimd.tensor_tensor(
                        out=o_sb[:, second_half], in0=o_sb[:, second_half], in1=bo_all[:, second_half], op=ALU.add
                    )
                group_rows = out_rows[j * GROUP : (j + 1) * GROUP, :].rearrange("(p i) n -> p i n", i=TILES)
                nc.sync.dma_start(out=group_rows[:, i, :], in_=o_sb[:])

            for step in range(-NORMALISE_AHEAD, N_TILES):
                if 0 <= step + NORMALISE_AHEAD < N_TILES:
                    normalise(step + NORMALISE_AHEAD)
                if 0 <= step + TRANSPOSE_AHEAD < N_TILES:
                    transpose_gn(step + TRANSPOSE_AHEAD)
                if 0 <= step + MULTIPLY_AHEAD < N_TILES:
                    multiply(step + MULTIPLY_AHEAD)
                if 0 <= step + PROJECT_AHEAD < N_TILES:
                    project(step + PROJECT_AHEAD)
                if 0 <= step:
                    add_bias_and_store(step)
                if 0 <= step + MULTIPLY_AHEAD < N_TILES and (step + MULTIPLY_AHEAD) % TILES == TILES - 1:
                    quantise_h((step + MULTIPLY_AHEAD) // TILES)
